import numpy as np
import ml_dtypes


def mxq(x, axis, fmt="e4m3"):
    dtype, down = {"e4m3": (ml_dtypes.float8_e4m3fn, 7), "e5m2": (ml_dtypes.float8_e5m2, 14)}[fmt]
    v = np.moveaxis(np.asarray(x, np.float32).astype(ml_dtypes.bfloat16).astype(np.float64), axis, -1)
    blocks = v.reshape(v.shape[:-1] + (-1, 32))
    amax = np.abs(blocks).max(-1, keepdims=True)
    byte = np.maximum(np.where(amax > 0, np.frexp(amax)[1] - 1 + 127, 0) - down, 1)
    scale = np.exp2(byte - 127.0)
    codes = (blocks / scale).astype(np.float32).astype(dtype).astype(np.float64)
    return np.moveaxis((codes * scale).reshape(v.shape), -1, axis)


WIDE = False


def mx_kscale(k):
    if not WIDE:
        return np.ones(k)
    levels = np.array([10, -10, 5, -5, 0])
    a = np.random.permutation(np.resize(levels, k // 512 * 4)).reshape(k // 512, 4)
    idx = np.arange(k)
    return np.exp2(a[idx // 512, idx % 128 // 32])


BF16 = ml_dtypes.bfloat16


def bf(x):
    return np.asarray(x, np.float32).astype(BF16)


def f64(x):
    return np.asarray(x).astype(np.float64)


B, T, C, HS, DW, DA, DV, DG = 4, 1024, 1024, 64, 512, 128, 128, 224


def softplus(z):
    return np.logaddexp(0.0, z)


def setup_inputs():
    s = mx_kscale(C)
    return {
        "x": bf(np.random.standard_normal((B, T, C)) * s),
        "x_w": bf(np.random.uniform(0.0, 1.0, C)),
        "w0": bf(np.random.standard_normal(C)),
        "w1": bf(np.random.standard_normal((C, DW)) / np.sqrt(C) / s[:, None]),
        "w2": bf(np.random.standard_normal((DW, C)) / np.sqrt(DW)),
    }


def reference(x, x_w, w0, w1, w2):
    x = f64(x)
    xprev = np.concatenate([np.zeros_like(x[:, :1]), x[:, :-1]], axis=1)
    xx = xprev - x
    xw = x + xx * f64(x_w)
    h = np.tanh(mxq(xw, 2, "e4m3") @ mxq(f64(w1), 0, "e4m3"))
    z = f64(w0) + (mxq(h, 2, "e4m3") @ mxq(f64(w2), 0, "e4m3"))
    return -softplus(-z) - 0.5

@@ -1,0 +1,260 @@
+import math
+
+from concourse import mybir
+from concourse.masks import make_identity
+
+F32 = mybir.dt.float32
+BF16 = mybir.dt.bfloat16
+U32 = mybir.dt.uint32
+U8 = mybir.dt.uint8
+FP8X4 = mybir.dt.float8_e4m3fn_x4
+ACT = mybir.ActivationFunctionType
+ALU = mybir.AluOpType
+
+P = 128
+PACK = 4
+B, T, C, DW = 4, 1024, 1024, 512
+C_BLOCKS = C // P
+K1_PASSES = C // (P * PACK)
+T_TILES = T // P
+T_GROUP = 512
+T_GROUPS = T // T_GROUP
+BANK = 512
+PAD = 8
+AHEAD = 2
+
+FLOPS = 2 * B * T * (C * DW + DW * C)
+
+
+def tile_full_tmix_params_pc_t_kernel(tc, x, x_w, w0, w1, w2, out):
+    nc = tc.nc
+    with tc.manual_schedule(), tc.tile_pool(name="keep", bufs=1) as keep, tc.tile_pool(
+        name="xin", bufs=2
+    ) as xin_pool, tc.tile_pool(name="codes", bufs=2) as codes_pool, tc.tile_pool(
+        name="res", bufs=4
+    ) as res_pool, tc.psum_pool(name="psx", bufs=3) as psum_x, tc.psum_pool(
+        name="psa", bufs=5
+    ) as psum_acc:
+        vectors = keep.tile([P, P], BF16, name="vectors")
+        nc.vector.memset(vectors[:], 0.0)
+        nc.sync.dma_start(out=vectors[0:C_BLOCKS, :], in_=x_w.rearrange("(r c) -> r c", c=P))
+        nc.sync.dma_start(
+            out=vectors[C_BLOCKS : 2 * C_BLOCKS, :], in_=w0.rearrange("(r c) -> r c", c=P)
+        )
+        w1_raw = keep.tile([P, K1_PASSES * PACK, DW], BF16, name="w1_raw")
+        nc.sync.dma_start(out=w1_raw[:], in_=w1.rearrange("(r p) n -> p r n", p=P))
+
+        x_tiles = {}
+
+        def load_x(b):
+            x_tiles[b] = xin_pool.tile([P, T_TILES, C], BF16, name="x_sb", tag="x_sb")
+            nc.sync.dma_start(out=x_tiles[b][:], in_=x[b].rearrange("(t p) c -> p t c", p=P))
+
+        load_x(0)
+        w2_raw = keep.tile([P, PACK, C], BF16, name="w2_raw")
+        nc.sync.dma_start(out=w2_raw[:], in_=w2.rearrange("(j p) c -> p j c", p=P))
+        load_x(1)
+
+        ident_bf = keep.tile([P, P], BF16, name="ident_bf")
+        make_identity(nc, ident_bf[:])
+        ident_f32 = keep.tile([P, P], F32, name="ident_f32")
+        make_identity(nc, ident_f32[:])
+
+        vectors_t = psum_acc.tile([P, P], BF16, name="vectors_t", tag="acc")
+        nc.tensor.transpose(out=vectors_t[:], in_=vectors[:], identity=ident_bf[:])
+        columns = keep.tile([P, 2 * C_BLOCKS], F32, name="columns")
+        nc.vector.tensor_copy(out=columns[:], in_=vectors_t[:, 0 : 2 * C_BLOCKS])
+        mix = columns[:, 0:C_BLOCKS]
+        bias = columns[:, C_BLOCKS : 2 * C_BLOCKS]
+        keep_share = keep.tile([P, C_BLOCKS], F32, name="keep_share")
+        nc.vector.tensor_scalar(
+            out=keep_share[:], in0=mix, scalar1=-1.0, scalar2=1.0, op0=ALU.mult, op1=ALU.add
+        )
+
+        w1_grouped = keep.tile([P, K1_PASSES, DW, PACK], BF16, name="w1_grouped", align_bytes=64)
+        w1_codes = keep.tile([P, K1_PASSES, DW], U32, name="w1_codes", align_bytes=64)
+        w1_scales = keep.tile([P, K1_PASSES, DW], U8, name="w1_scales", align_bytes=64)
+        for g in range(K1_PASSES):
+            nc.scalar.copy(
+                out=w1_grouped[:, g],
+                in_=w1_raw[:, PACK * g : PACK * (g + 1), :].rearrange("p j n -> p n j"),
+            )
+        for g in range(K1_PASSES):
+            nc.vector.quantize_mx(
+                out=w1_codes[:, g, :].bitcast(FP8X4),
+                scales=w1_scales[:, g, :],
+                in_=w1_grouped[:, g].rearrange("p n j -> p (n j)"),
+            )
+        w2_grouped = keep.tile([P, C, PACK], BF16, name="w2_grouped", align_bytes=64)
+        w2_codes = keep.tile([P, C], U32, name="w2_codes", align_bytes=64)
+        w2_scales = keep.tile([P, C], U8, name="w2_scales", align_bytes=64)
+
+        carried = keep.tile([P, C_BLOCKS, PAD + T], F32, name="carried")
+        nc.vector.memset(carried[:, :, 0:PAD], 0.0)
+        planes = keep.tile([P, C_BLOCKS, T], BF16, name="planes")
+        grouped = keep.tile([P, K1_PASSES, T, PACK], BF16, name="grouped", align_bytes=64)
+        xt_tiles = {}
+        xw_codes = {}
+        xw_scales = {}
+
+        def transpose_block(q):
+            b, cb = divmod(q, C_BLOCKS)
+            if b >= B:
+                return
+            xt_tiles[q] = psum_x.tile([P, T], BF16, name="xt", tag="xt")
+            for t in range(T_TILES):
+                nc.tensor.transpose(
+                    out=xt_tiles[q][:, P * t : P * (t + 1)],
+                    in_=x_tiles[b][:, t, P * cb : P * (cb + 1)],
+                    identity=ident_bf[:],
+                )
+
+        def mix_block(q):
+            b, cb = divmod(q, C_BLOCKS)
+            if b >= B:
+                return
+            transpose_block(q + AHEAD)
+            xt = xt_tiles[q]
+            if b == 0:
+                nc.scalar.activation(
+                    out=carried[:, cb, PAD : PAD + T], in_=xt[:], func=ACT.Copy,
+                    scale=mix[:, cb : cb + 1],
+                )
+            else:
+                nc.vector.tensor_scalar(
+                    out=carried[:, cb, PAD : PAD + T], in0=xt[:], scalar1=mix[:, cb : cb + 1],
+                    scalar2=None, op0=ALU.mult,
+                )
+            nc.vector.scalar_tensor_tensor(
+                out=planes[:, cb, :], in0=xt[:], scalar=keep_share[:, cb : cb + 1],
+                in1=carried[:, cb, PAD - 1 : PAD - 1 + T], op0=ALU.mult, op1=ALU.add,
+            )
+            if cb % PACK == PACK - 1:
+                g = cb // PACK
+                if g == 0:
+                    xw_codes[b] = codes_pool.tile(
+                        [P, K1_PASSES, T], U32, name="xw_codes", tag="xw_codes", align_bytes=64
+                    )
+                    xw_scales[b] = codes_pool.tile(
+                        [P, K1_PASSES, T], U8, name="xw_scales", tag="xw_scales", align_bytes=64
+                    )
+                nc.vector.tensor_copy(
+                    out=grouped[:, g].rearrange("p (c i) j -> p c j i", i=4),
+                    in_=planes[:, PACK * g : PACK * (g + 1), :].rearrange(
+                        "p j (c i) -> p c j i", i=4
+                    ),
+                )
+                nc.vector.quantize_mx(
+                    out=xw_codes[b][:, g, :].bitcast(FP8X4),
+                    scales=xw_scales[b][:, g, :],
+                    in_=grouped[:, g].rearrange("p c j -> p (c j)"),
+                )
+
+        h_grouped = {}
+        h_codes = {}
+        h_scales = {}
+        gate = keep.tile([P, C_BLOCKS, T], F32, name="gate")
+        table_warm = keep.tile([P, 1], F32, name="table_warm")
+
+        def hidden(b, t):
+            tg, i = divmod(t, T_GROUP // P)
+            if i == 0:
+                h_grouped[tg] = codes_pool.tile(
+                    [P, T_GROUP, PACK], BF16, name="h_grouped", tag="h_grouped", align_bytes=64
+                )
+            acc = psum_acc.tile([P, PACK, P], F32, name="h_acc", tag="acc")
+            tokens = slice(P * t, P * (t + 1))
+            for m in range(PACK):
+                for g in range(K1_PASSES):
+                    nc.tensor.matmul_mx(
+                        out=acc[:, m, :],
+                        lhsT=w1_codes[:, g, P * m : P * (m + 1)].bitcast(FP8X4),
+                        lhsT_scale=w1_scales[:, g, P * m : P * (m + 1)],
+                        rhs=xw_codes[b][:, g, tokens].bitcast(FP8X4),
+                        rhs_scale=xw_scales[b][:, g, tokens],
+                        start=(g == 0),
+                        stop=(g == K1_PASSES - 1),
+                    )
+            nc.scalar.activation(
+                out=h_grouped[tg][:, P * i : P * (i + 1), :],
+                in_=acc[:].rearrange("p m t -> p t m"),
+                func=ACT.Tanh,
+            )
+
+        def quantise_hidden(tg):
+            h_codes[tg] = codes_pool.tile(
+                [P, T_GROUP], U32, name="h_codes", tag="h_codes", align_bytes=64
+            )
+            h_scales[tg] = codes_pool.tile(
+                [P, T_GROUP], U8, name="h_scales", tag="h_scales", align_bytes=64
+            )
+            nc.vector.quantize_mx(
+                out=h_codes[tg][:].bitcast(FP8X4),
+                scales=h_scales[tg][:],
+                in_=h_grouped[tg][:].rearrange("p t j -> p (t j)"),
+            )
+
+        def gates(tg, cs):
+            acc = psum_acc.tile([P, T_GROUP], F32, name="z_acc", tag="acc")
+            nc.tensor.matmul_mx(
+                out=acc[:],
+                lhsT=w2_codes[:, P * cs : P * (cs + 1)].bitcast(FP8X4),
+                lhsT_scale=w2_scales[:, P * cs : P * (cs + 1)],
+                rhs=h_codes[tg][:].bitcast(FP8X4),
+                rhs_scale=h_scales[tg][:],
+                start=True,
+                stop=True,
+            )
+            nc.scalar.activation(
+                out=gate[:, cs, T_GROUP * tg : T_GROUP * (tg + 1)], in_=acc[:], func=ACT.Sigmoid,
+                bias=bias[:, cs : cs + 1], scale=1.0,
+            )
+
+        def output(b, t):
+            result = res_pool.tile([P, C], F32, name="result", tag="result")
+            for half in range(C // BANK):
+                acc = psum_acc.tile([P, BANK], F32, name="o_acc", tag="acc")
+                for i in range(BANK // P):
+                    nc.tensor.transpose(
+                        out=acc[:, P * i : P * (i + 1)],
+                        in_=gate[:, (BANK // P) * half + i, P * t : P * (t + 1)],
+                        identity=ident_f32[:],
+                    )
+                nc.scalar.activation(
+                    out=result[:, BANK * half : BANK * (half + 1)], in_=acc[:], func=ACT.Ln,
+                    scale=math.exp(-0.5),
+                )
+            nc.sync.dma_start(out=out[b, P * t : P * (t + 1), :], in_=result[:])
+
+        for q in range(AHEAD):
+            transpose_block(q)
+        for q in range(C_BLOCKS):
+            mix_block(q)
+        nc.scalar.copy(out=w2_grouped[:], in_=w2_raw[:].rearrange("p j c -> p c j"))
+        nc.vector.quantize_mx(
+            out=w2_codes[:].bitcast(FP8X4),
+            scales=w2_scales[:],
+            in_=w2_grouped[:].rearrange("p c j -> p (c j)"),
+        )
+
+        for b in range(B):
+            following = C_BLOCKS * (b + 1)
+            if b + 2 < B:
+                load_x(b + 2)
+            nc.scalar.activation(out=table_warm[:], in_=columns[:, 0:1], func=ACT.Sigmoid)
+            for t in range(T_TILES):
+                hidden(b, t)
+                if t % 4 == 3:
+                    mix_block(following + t // 4)
+            quantise_hidden(0)
+            for cs in range(C_BLOCKS):
+                gates(0, cs)
+            mix_block(following + 2)
+            quantise_hidden(1)
+            for cs in range(C_BLOCKS):
+                gates(1, cs)
+            mix_block(following + 3)
+            for t in range(T_TILES):
+                output(b, t)
+                if t % 2 == 1:
+                    mix_block(following + 4 + t // 2)

@@ -21,6 +21,7 @@ T_GROUP = 512
 T_GROUPS = T // T_GROUP
 BANK = 512
 PAD = 8
+X_PIECE = 2 * P
 AHEAD = 2
 
 FLOPS = 2 * B * T * (C * DW + DW * C)
@@ -31,7 +32,7 @@ def tile_full_tmix_params_pc_t_kernel(tc, x, x_w, w0, w1, w2, out):
     with tc.manual_schedule(), tc.tile_pool(name="keep", bufs=1) as keep, tc.tile_pool(
         name="xin", bufs=2
     ) as xin_pool, tc.tile_pool(name="codes", bufs=2) as codes_pool, tc.tile_pool(
-        name="res", bufs=4
+        name="res", bufs=6
     ) as res_pool, tc.psum_pool(name="psx", bufs=3) as psum_x, tc.psum_pool(
         name="psa", bufs=5
     ) as psum_acc:
@@ -41,16 +42,19 @@ def tile_full_tmix_params_pc_t_kernel(tc, x, x_w, w0, w1, w2, out):
         nc.sync.dma_start(
             out=vectors[C_BLOCKS : 2 * C_BLOCKS, :], in_=w0.rearrange("(r c) -> r c", c=P)
         )
-        w1_raw = keep.tile([P, K1_PASSES * PACK, DW], BF16, name="w1_raw")
-        nc.sync.dma_start(out=w1_raw[:], in_=w1.rearrange("(r p) n -> p r n", p=P))
-
         x_tiles = {}
 
         def load_x(b):
             x_tiles[b] = xin_pool.tile([P, T_TILES, C], BF16, name="x_sb", tag="x_sb")
-            nc.sync.dma_start(out=x_tiles[b][:], in_=x[b].rearrange("(t p) c -> p t c", p=P))
+            rows = x[b].rearrange("(t p) c -> p t c", p=P)
+            for c0 in range(0, C, X_PIECE):
+                nc.sync.dma_start(
+                    out=x_tiles[b][:, :, c0 : c0 + X_PIECE], in_=rows[:, :, c0 : c0 + X_PIECE]
+                )
 
         load_x(0)
+        w1_raw = keep.tile([P, K1_PASSES * PACK, DW], BF16, name="w1_raw")
+        nc.sync.dma_start(out=w1_raw[:], in_=w1.rearrange("(r p) n -> p r n", p=P))
         w2_raw = keep.tile([P, PACK, C], BF16, name="w2_raw")
         nc.sync.dma_start(out=w2_raw[:], in_=w2.rearrange("(j p) c -> p j c", p=P))
         load_x(1)
@@ -74,17 +78,6 @@ def tile_full_tmix_params_pc_t_kernel(tc, x, x_w, w0, w1, w2, out):
         w1_grouped = keep.tile([P, K1_PASSES, DW, PACK], BF16, name="w1_grouped", align_bytes=64)
         w1_codes = keep.tile([P, K1_PASSES, DW], U32, name="w1_codes", align_bytes=64)
         w1_scales = keep.tile([P, K1_PASSES, DW], U8, name="w1_scales", align_bytes=64)
-        for g in range(K1_PASSES):
-            nc.scalar.copy(
-                out=w1_grouped[:, g],
-                in_=w1_raw[:, PACK * g : PACK * (g + 1), :].rearrange("p j n -> p n j"),
-            )
-        for g in range(K1_PASSES):
-            nc.vector.quantize_mx(
-                out=w1_codes[:, g, :].bitcast(FP8X4),
-                scales=w1_scales[:, g, :],
-                in_=w1_grouped[:, g].rearrange("p n j -> p (n j)"),
-            )
         w2_grouped = keep.tile([P, C, PACK], BF16, name="w2_grouped", align_bytes=64)
         w2_codes = keep.tile([P, C], U32, name="w2_codes", align_bytes=64)
         w2_scales = keep.tile([P, C], U8, name="w2_scales", align_bytes=64)
@@ -138,17 +131,24 @@ def tile_full_tmix_params_pc_t_kernel(tc, x, x_w, w0, w1, w2, out):
                     xw_scales[b] = codes_pool.tile(
                         [P, K1_PASSES, T], U8, name="xw_scales", tag="xw_scales", align_bytes=64
                     )
-                nc.vector.tensor_copy(
-                    out=grouped[:, g].rearrange("p (c i) j -> p c j i", i=4),
-                    in_=planes[:, PACK * g : PACK * (g + 1), :].rearrange(
-                        "p j (c i) -> p c j i", i=4
-                    ),
-                )
-                nc.vector.quantize_mx(
-                    out=xw_codes[b][:, g, :].bitcast(FP8X4),
-                    scales=xw_scales[b][:, g, :],
-                    in_=grouped[:, g].rearrange("p c j -> p (c j)"),
-                )
+                    nc.gpsimd.tensor_scalar(
+                        out=grouped[:, g],
+                        in0=planes[:, PACK * g : PACK * (g + 1), :].rearrange("p j t -> p t j"),
+                        scalar1=1.0, scalar2=0.0, op0=ALU.mult, op1=ALU.add,
+                    )
+                else:
+                    nc.vector.tensor_copy(
+                        out=grouped[:, g].rearrange("p (c i) j -> p c j i", i=4),
+                        in_=planes[:, PACK * g : PACK * (g + 1), :].rearrange(
+                            "p j (c i) -> p c j i", i=4
+                        ),
+                    )
+                    for gq in range(K1_PASSES):
+                        nc.vector.quantize_mx(
+                            out=xw_codes[b][:, gq, :].bitcast(FP8X4),
+                            scales=xw_scales[b][:, gq, :],
+                            in_=grouped[:, gq].rearrange("p c j -> p (c j)"),
+                        )
 
         h_grouped = {}
         h_codes = {}
@@ -211,8 +211,8 @@ def tile_full_tmix_params_pc_t_kernel(tc, x, x_w, w0, w1, w2, out):
             )
 
         def output(b, t):
-            result = res_pool.tile([P, C], F32, name="result", tag="result")
             for half in range(C // BANK):
+                result = res_pool.tile([P, BANK], F32, name="result", tag="result")
                 acc = psum_acc.tile([P, BANK], F32, name="o_acc", tag="acc")
                 for i in range(BANK // P):
                     nc.tensor.transpose(
@@ -221,16 +221,31 @@ def tile_full_tmix_params_pc_t_kernel(tc, x, x_w, w0, w1, w2, out):
                         identity=ident_f32[:],
                     )
                 nc.scalar.activation(
-                    out=result[:, BANK * half : BANK * (half + 1)], in_=acc[:], func=ACT.Ln,
-                    scale=math.exp(-0.5),
+                    out=result[:], in_=acc[:], func=ACT.Ln, scale=math.exp(-0.5)
                 )
-            nc.sync.dma_start(out=out[b, P * t : P * (t + 1), :], in_=result[:])
+                nc.sync.dma_start(
+                    out=out[b, P * t : P * (t + 1), BANK * half : BANK * (half + 1)],
+                    in_=result[:],
+                )
 
         for q in range(AHEAD):
             transpose_block(q)
         for q in range(C_BLOCKS):
             mix_block(q)
-        nc.scalar.copy(out=w2_grouped[:], in_=w2_raw[:].rearrange("p j c -> p c j"))
+        for g in range(K1_PASSES):
+            nc.scalar.copy(
+                out=w1_grouped[:, g],
+                in_=w1_raw[:, PACK * g : PACK * (g + 1), :].rearrange("p j n -> p n j"),
+            )
+            nc.vector.quantize_mx(
+                out=w1_codes[:, g, :].bitcast(FP8X4),
+                scales=w1_scales[:, g, :],
+                in_=w1_grouped[:, g].rearrange("p n j -> p (n j)"),
+            )
+        nc.gpsimd.tensor_scalar(
+            out=w2_grouped[:], in0=w2_raw[:].rearrange("p j c -> p c j"),
+            scalar1=1.0, scalar2=0.0, op0=ALU.mult, op1=ALU.add,
+        )
         nc.vector.quantize_mx(
             out=w2_codes[:].bitcast(FP8X4),
             scales=w2_scales[:],

@@ -32,7 +32,7 @@ def tile_full_tmix_params_pc_t_kernel(tc, x, x_w, w0, w1, w2, out):
     with tc.manual_schedule(), tc.tile_pool(name="keep", bufs=1) as keep, tc.tile_pool(
         name="xin", bufs=2
     ) as xin_pool, tc.tile_pool(name="codes", bufs=2) as codes_pool, tc.tile_pool(
-        name="res", bufs=6
+        name="res", bufs=12
     ) as res_pool, tc.psum_pool(name="psx", bufs=3) as psum_x, tc.psum_pool(
         name="psa", bufs=5
     ) as psum_acc:
@@ -242,9 +242,9 @@ def tile_full_tmix_params_pc_t_kernel(tc, x, x_w, w0, w1, w2, out):
                 scales=w1_scales[:, g, :],
                 in_=w1_grouped[:, g].rearrange("p n j -> p (n j)"),
             )
-        nc.gpsimd.tensor_scalar(
-            out=w2_grouped[:], in0=w2_raw[:].rearrange("p j c -> p c j"),
-            scalar1=1.0, scalar2=0.0, op0=ALU.mult, op1=ALU.add,
+        nc.vector.tensor_copy(
+            out=w2_grouped[:].rearrange("p (c i) j -> p c j i", i=4),
+            in_=w2_raw[:].rearrange("p j (c i) -> p c j i", i=4),
         )
         nc.vector.quantize_mx(
             out=w2_codes[:].bitcast(FP8X4),

@@ -22,7 +22,9 @@ T_GROUPS = T // T_GROUP
 BANK = 512
 PAD = 8
 X_PIECE = 2 * P
-AHEAD = 2
+LEAD = 2
+SCALAR_BANKS = T_TILES + T_GROUPS * C_BLOCKS
+BANKS_A_BLOCK = SCALAR_BANKS // C_BLOCKS
 
 FLOPS = 2 * B * T * (C * DW + DW * C)
 
@@ -33,8 +35,8 @@ def tile_full_tmix_params_pc_t_kernel(tc, x, x_w, w0, w1, w2, out):
         name="xin", bufs=2
     ) as xin_pool, tc.tile_pool(name="codes", bufs=2) as codes_pool, tc.tile_pool(
         name="res", bufs=12
-    ) as res_pool, tc.psum_pool(name="psx", bufs=3) as psum_x, tc.psum_pool(
-        name="psa", bufs=5
+    ) as res_pool, tc.psum_pool(name="psx", bufs=4) as psum_x, tc.psum_pool(
+        name="psa", bufs=4
     ) as psum_acc:
         vectors = keep.tile([P, P], BF16, name="vectors")
         nc.vector.memset(vectors[:], 0.0)
@@ -106,7 +108,6 @@ def tile_full_tmix_params_pc_t_kernel(tc, x, x_w, w0, w1, w2, out):
             b, cb = divmod(q, C_BLOCKS)
             if b >= B:
                 return
-            transpose_block(q + AHEAD)
             xt = xt_tiles[q]
             if b == 0:
                 nc.scalar.activation(
@@ -228,9 +229,10 @@ def tile_full_tmix_params_pc_t_kernel(tc, x, x_w, w0, w1, w2, out):
                     in_=result[:],
                 )
 
-        for q in range(AHEAD):
+        for q in range(LEAD):
             transpose_block(q)
         for q in range(C_BLOCKS):
+            transpose_block(q + LEAD)
             mix_block(q)
         for g in range(K1_PASSES):
             nc.scalar.copy(
@@ -252,24 +254,27 @@ def tile_full_tmix_params_pc_t_kernel(tc, x, x_w, w0, w1, w2, out):
             in_=w2_grouped[:].rearrange("p c j -> p (c j)"),
         )
 
+        for q in range(C_BLOCKS, C_BLOCKS + LEAD):
+            mix_block(q)
+
+        def mix_behind(b, bank):
+            if bank % BANKS_A_BLOCK == BANKS_A_BLOCK - 1:
+                q = C_BLOCKS * (b + 1) + LEAD + bank // BANKS_A_BLOCK
+                transpose_block(q)
+                mix_block(q)
+
         for b in range(B):
-            following = C_BLOCKS * (b + 1)
             if b + 2 < B:
                 load_x(b + 2)
             nc.scalar.activation(out=table_warm[:], in_=columns[:, 0:1], func=ACT.Sigmoid)
             for t in range(T_TILES):
                 hidden(b, t)
-                if t % 4 == 3:
-                    mix_block(following + t // 4)
-            quantise_hidden(0)
-            for cs in range(C_BLOCKS):
-                gates(0, cs)
-            mix_block(following + 2)
-            quantise_hidden(1)
-            for cs in range(C_BLOCKS):
-                gates(1, cs)
-            mix_block(following + 3)
+                if t % (T_GROUP // P) == T_GROUP // P - 1:
+                    quantise_hidden(t // (T_GROUP // P))
+                mix_behind(b, t)
+            for tg in range(T_GROUPS):
+                for cs in range(C_BLOCKS):
+                    gates(tg, cs)
+                    mix_behind(b, T_TILES + C_BLOCKS * tg + cs)
             for t in range(T_TILES):
                 output(b, t)
-                if t % 2 == 1:
-                    mix_block(following + 4 + t // 2)

@@ -22,6 +22,7 @@ T_GROUPS = T // T_GROUP
 BANK = 512
 PAD = 8
 X_PIECE = 2 * P
+X_BANKS = 4
 LEAD = 2
 SCALAR_BANKS = T_TILES + T_GROUPS * C_BLOCKS
 BANKS_A_BLOCK = SCALAR_BANKS // C_BLOCKS
@@ -34,8 +35,8 @@ def tile_full_tmix_params_pc_t_kernel(tc, x, x_w, w0, w1, w2, out):
     with tc.manual_schedule(), tc.tile_pool(name="keep", bufs=1) as keep, tc.tile_pool(
         name="xin", bufs=2
     ) as xin_pool, tc.tile_pool(name="codes", bufs=2) as codes_pool, tc.tile_pool(
-        name="res", bufs=12
-    ) as res_pool, tc.psum_pool(name="psx", bufs=4) as psum_x, tc.psum_pool(
+        name="res", bufs=2
+    ) as res_pool, tc.psum_pool(name="psx", bufs=X_BANKS) as psum_x, tc.psum_pool(
         name="psa", bufs=4
     ) as psum_acc:
         vectors = keep.tile([P, P], BF16, name="vectors")
@@ -84,7 +85,7 @@ def tile_full_tmix_params_pc_t_kernel(tc, x, x_w, w0, w1, w2, out):
         w2_codes = keep.tile([P, C], U32, name="w2_codes", align_bytes=64)
         w2_scales = keep.tile([P, C], U8, name="w2_scales", align_bytes=64)
 
-        carried = keep.tile([P, C_BLOCKS, PAD + T], F32, name="carried")
+        carried = keep.tile([P, X_BANKS, PAD + T], F32, name="carried")
         nc.vector.memset(carried[:, :, 0:PAD], 0.0)
         planes = keep.tile([P, C_BLOCKS, T], BF16, name="planes")
         grouped = keep.tile([P, K1_PASSES, T, PACK], BF16, name="grouped", align_bytes=64)
@@ -109,19 +110,20 @@ def tile_full_tmix_params_pc_t_kernel(tc, x, x_w, w0, w1, w2, out):
             if b >= B:
                 return
             xt = xt_tiles[q]
+            late = carried[:, q % X_BANKS, :]
             if b == 0:
                 nc.scalar.activation(
-                    out=carried[:, cb, PAD : PAD + T], in_=xt[:], func=ACT.Copy,
+                    out=late[:, PAD : PAD + T], in_=xt[:], func=ACT.Copy,
                     scale=mix[:, cb : cb + 1],
                 )
             else:
                 nc.vector.tensor_scalar(
-                    out=carried[:, cb, PAD : PAD + T], in0=xt[:], scalar1=mix[:, cb : cb + 1],
+                    out=late[:, PAD : PAD + T], in0=xt[:], scalar1=mix[:, cb : cb + 1],
                     scalar2=None, op0=ALU.mult,
                 )
             nc.vector.scalar_tensor_tensor(
                 out=planes[:, cb, :], in0=xt[:], scalar=keep_share[:, cb : cb + 1],
-                in1=carried[:, cb, PAD - 1 : PAD - 1 + T], op0=ALU.mult, op1=ALU.add,
+                in1=late[:, PAD - 1 : PAD - 1 + T], op0=ALU.mult, op1=ALU.add,
             )
             if cb % PACK == PACK - 1:
                 g = cb // PACK
@@ -211,9 +213,14 @@ def tile_full_tmix_params_pc_t_kernel(tc, x, x_w, w0, w1, w2, out):
                 bias=bias[:, cs : cs + 1], scale=1.0,
             )
 
+        results = {}
+
         def output(b, t):
+            tg, i = divmod(t, T_GROUP // P)
+            if i == 0:
+                results[tg] = res_pool.tile([P, T_GROUP // P, C], F32, name="result", tag="result")
             for half in range(C // BANK):
-                result = res_pool.tile([P, BANK], F32, name="result", tag="result")
+                result = results[tg][:, i, BANK * half : BANK * (half + 1)]
                 acc = psum_acc.tile([P, BANK], F32, name="o_acc", tag="acc")
                 for i in range(BANK // P):
                     nc.tensor.transpose(
@@ -221,12 +228,10 @@ def tile_full_tmix_params_pc_t_kernel(tc, x, x_w, w0, w1, w2, out):
                         in_=gate[:, (BANK // P) * half + i, P * t : P * (t + 1)],
                         identity=ident_f32[:],
                     )
-                nc.scalar.activation(
-                    out=result[:], in_=acc[:], func=ACT.Ln, scale=math.exp(-0.5)
-                )
+                nc.scalar.activation(out=result, in_=acc[:], func=ACT.Ln, scale=math.exp(-0.5))
                 nc.sync.dma_start(
                     out=out[b, P * t : P * (t + 1), BANK * half : BANK * (half + 1)],
-                    in_=result[:],
+                    in_=result,
                 )
 
         for q in range(LEAD):

@@ -23,7 +23,7 @@ BANK = 512
 PAD = 8
 X_PIECE = 2 * P
 X_BANKS = 4
-LEAD = 2
+LEAD = 1
 SCALAR_BANKS = T_TILES + T_GROUPS * C_BLOCKS
 BANKS_A_BLOCK = SCALAR_BANKS // C_BLOCKS
 
@@ -35,7 +35,7 @@ def tile_full_tmix_params_pc_t_kernel(tc, x, x_w, w0, w1, w2, out):
     with tc.manual_schedule(), tc.tile_pool(name="keep", bufs=1) as keep, tc.tile_pool(
         name="xin", bufs=2
     ) as xin_pool, tc.tile_pool(name="codes", bufs=2) as codes_pool, tc.tile_pool(
-        name="res", bufs=2
+        name="res", bufs=8
     ) as res_pool, tc.psum_pool(name="psx", bufs=X_BANKS) as psum_x, tc.psum_pool(
         name="psa", bufs=4
     ) as psum_acc:
@@ -139,19 +139,22 @@ def tile_full_tmix_params_pc_t_kernel(tc, x, x_w, w0, w1, w2, out):
                         in0=planes[:, PACK * g : PACK * (g + 1), :].rearrange("p j t -> p t j"),
                         scalar1=1.0, scalar2=0.0, op0=ALU.mult, op1=ALU.add,
                     )
-                else:
-                    nc.vector.tensor_copy(
-                        out=grouped[:, g].rearrange("p (c i) j -> p c j i", i=4),
-                        in_=planes[:, PACK * g : PACK * (g + 1), :].rearrange(
-                            "p j (c i) -> p c j i", i=4
-                        ),
-                    )
-                    for gq in range(K1_PASSES):
-                        nc.vector.quantize_mx(
-                            out=xw_codes[b][:, gq, :].bitcast(FP8X4),
-                            scales=xw_scales[b][:, gq, :],
-                            in_=grouped[:, gq].rearrange("p c j -> p (c j)"),
-                        )
+                elif b > 0:
+                    for tg in range(T_GROUPS):
+                        pack(b, tg)
+
+        def pack(b, tg):
+            tokens = slice(T_GROUP * tg, T_GROUP * (tg + 1))
+            nc.vector.tensor_copy(
+                out=grouped[:, 1, tokens, :].rearrange("p (c i) j -> p c j i", i=4),
+                in_=planes[:, PACK : 2 * PACK, tokens].rearrange("p j (c i) -> p c j i", i=4),
+            )
+            for g in range(K1_PASSES):
+                nc.vector.quantize_mx(
+                    out=xw_codes[b][:, g, tokens].bitcast(FP8X4),
+                    scales=xw_scales[b][:, g, tokens],
+                    in_=grouped[:, g, tokens, :].rearrange("p c j -> p (c j)"),
+                )
 
         h_grouped = {}
         h_codes = {}
@@ -213,14 +216,9 @@ def tile_full_tmix_params_pc_t_kernel(tc, x, x_w, w0, w1, w2, out):
                 bias=bias[:, cs : cs + 1], scale=1.0,
             )
 
-        results = {}
-
         def output(b, t):
-            tg, i = divmod(t, T_GROUP // P)
-            if i == 0:
-                results[tg] = res_pool.tile([P, T_GROUP // P, C], F32, name="result", tag="result")
+            result = res_pool.tile([P, C], F32, name="result", tag="result")
             for half in range(C // BANK):
-                result = results[tg][:, i, BANK * half : BANK * (half + 1)]
                 acc = psum_acc.tile([P, BANK], F32, name="o_acc", tag="acc")
                 for i in range(BANK // P):
                     nc.tensor.transpose(
@@ -228,17 +226,18 @@ def tile_full_tmix_params_pc_t_kernel(tc, x, x_w, w0, w1, w2, out):
                         in_=gate[:, (BANK // P) * half + i, P * t : P * (t + 1)],
                         identity=ident_f32[:],
                     )
-                nc.scalar.activation(out=result, in_=acc[:], func=ACT.Ln, scale=math.exp(-0.5))
-                nc.sync.dma_start(
-                    out=out[b, P * t : P * (t + 1), BANK * half : BANK * (half + 1)],
-                    in_=result,
+                nc.scalar.activation(
+                    out=result[:, BANK * half : BANK * (half + 1)], in_=acc[:], func=ACT.Ln,
+                    scale=math.exp(-0.5),
                 )
+            nc.sync.dma_start(out=out[b, P * t : P * (t + 1), :], in_=result[:])
 
         for q in range(LEAD):
             transpose_block(q)
         for q in range(C_BLOCKS):
             transpose_block(q + LEAD)
             mix_block(q)
+        pack(0, 0)
         for g in range(K1_PASSES):
             nc.scalar.copy(
                 out=w1_grouped[:, g],
@@ -249,6 +248,7 @@ def tile_full_tmix_params_pc_t_kernel(tc, x, x_w, w0, w1, w2, out):
                 scales=w1_scales[:, g, :],
                 in_=w1_grouped[:, g].rearrange("p n j -> p (n j)"),
             )
+        pack(0, 1)
         nc.vector.tensor_copy(
             out=w2_grouped[:].rearrange("p (c i) j -> p c j i", i=4),
             in_=w2_raw[:].rearrange("p j (c i) -> p c j i", i=4),
@@ -259,14 +259,11 @@ def tile_full_tmix_params_pc_t_kernel(tc, x, x_w, w0, w1, w2, out):
             in_=w2_grouped[:].rearrange("p c j -> p (c j)"),
         )
 
-        for q in range(C_BLOCKS, C_BLOCKS + LEAD):
-            mix_block(q)
-
         def mix_behind(b, bank):
             if bank % BANKS_A_BLOCK == BANKS_A_BLOCK - 1:
                 q = C_BLOCKS * (b + 1) + LEAD + bank // BANKS_A_BLOCK
                 transpose_block(q)
-                mix_block(q)
+                mix_block(q - LEAD if b == 0 else q)
 
         for b in range(B):
             if b + 2 < B:
@@ -281,5 +278,8 @@ def tile_full_tmix_params_pc_t_kernel(tc, x, x_w, w0, w1, w2, out):
                 for cs in range(C_BLOCKS):
                     gates(tg, cs)
                     mix_behind(b, T_TILES + C_BLOCKS * tg + cs)
+            if b == 0:
+                for q in range(2 * C_BLOCKS, 2 * C_BLOCKS + LEAD):
+                    mix_block(q)
             for t in range(T_TILES):
                 output(b, t)

@@ -22,7 +22,11 @@ T_GROUPS = T // T_GROUP
 BANK = 512
 PAD = 8
 X_PIECE = 2 * P
+RING = 8
 X_BANKS = 4
+TANH_PLACES = (1, 3)
+GATE_PLACES = (1, 3, 5, 7)
+OUT_PLACES = (0, 2)
 LEAD = 1
 SCALAR_BANKS = T_TILES + T_GROUPS * C_BLOCKS
 BANKS_A_BLOCK = SCALAR_BANKS // C_BLOCKS
@@ -35,10 +39,13 @@ def tile_full_tmix_params_pc_t_kernel(tc, x, x_w, w0, w1, w2, out):
     with tc.manual_schedule(), tc.tile_pool(name="keep", bufs=1) as keep, tc.tile_pool(
         name="xin", bufs=2
     ) as xin_pool, tc.tile_pool(name="codes", bufs=2) as codes_pool, tc.tile_pool(
-        name="res", bufs=8
+        name="res", bufs=7
     ) as res_pool, tc.psum_pool(name="psx", bufs=X_BANKS) as psum_x, tc.psum_pool(
         name="psa", bufs=4
     ) as psum_acc:
+        table_warm = keep.tile([P, 1], F32, name="table_warm")
+        nc.vector.memset(table_warm[:], 0.0)
+        nc.scalar.activation(out=table_warm[:], in_=table_warm[:], func=ACT.Sigmoid)
         vectors = keep.tile([P, P], BF16, name="vectors")
         nc.vector.memset(vectors[:], 0.0)
         nc.sync.dma_start(out=vectors[0:C_BLOCKS, :], in_=x_w.rearrange("(r c) -> r c", c=P))
@@ -47,17 +54,19 @@ def tile_full_tmix_params_pc_t_kernel(tc, x, x_w, w0, w1, w2, out):
         )
         x_tiles = {}
 
-        def load_x(b):
-            x_tiles[b] = xin_pool.tile([P, T_TILES, C], BF16, name="x_sb", tag="x_sb")
+        def load_x(b, t0=0, t1=T_TILES, piece=C // 2):
+            if t0 == 0:
+                x_tiles[b] = xin_pool.tile([P, T_TILES, C], BF16, name="x_sb", tag="x_sb")
             rows = x[b].rearrange("(t p) c -> p t c", p=P)
-            for c0 in range(0, C, X_PIECE):
+            for c0 in range(0, C, piece):
                 nc.sync.dma_start(
-                    out=x_tiles[b][:, :, c0 : c0 + X_PIECE], in_=rows[:, :, c0 : c0 + X_PIECE]
+                    out=x_tiles[b][:, t0:t1, c0 : c0 + piece], in_=rows[:, t0:t1, c0 : c0 + piece]
                 )
 
-        load_x(0)
+        load_x(0, 0, T_TILES // 2, X_PIECE)
         w1_raw = keep.tile([P, K1_PASSES * PACK, DW], BF16, name="w1_raw")
         nc.sync.dma_start(out=w1_raw[:], in_=w1.rearrange("(r p) n -> p r n", p=P))
+        load_x(0, T_TILES // 2, T_TILES)
         w2_raw = keep.tile([P, PACK, C], BF16, name="w2_raw")
         nc.sync.dma_start(out=w2_raw[:], in_=w2.rearrange("(j p) c -> p j c", p=P))
         load_x(1)
@@ -85,7 +94,7 @@ def tile_full_tmix_params_pc_t_kernel(tc, x, x_w, w0, w1, w2, out):
         w2_codes = keep.tile([P, C], U32, name="w2_codes", align_bytes=64)
         w2_scales = keep.tile([P, C], U8, name="w2_scales", align_bytes=64)
 
-        carried = keep.tile([P, X_BANKS, PAD + T], F32, name="carried")
+        carried = keep.tile([P, RING, PAD + T], F32, name="carried")
         nc.vector.memset(carried[:, :, 0:PAD], 0.0)
         planes = keep.tile([P, C_BLOCKS, T], BF16, name="planes")
         grouped = keep.tile([P, K1_PASSES, T, PACK], BF16, name="grouped", align_bytes=64)
@@ -110,17 +119,11 @@ def tile_full_tmix_params_pc_t_kernel(tc, x, x_w, w0, w1, w2, out):
             if b >= B:
                 return
             xt = xt_tiles[q]
-            late = carried[:, q % X_BANKS, :]
-            if b == 0:
-                nc.scalar.activation(
-                    out=late[:, PAD : PAD + T], in_=xt[:], func=ACT.Copy,
-                    scale=mix[:, cb : cb + 1],
-                )
-            else:
-                nc.vector.tensor_scalar(
-                    out=late[:, PAD : PAD + T], in0=xt[:], scalar1=mix[:, cb : cb + 1],
-                    scalar2=None, op0=ALU.mult,
-                )
+            late = carried[:, q % RING, :]
+            nc.vector.tensor_scalar(
+                out=late[:, PAD : PAD + T], in0=xt[:], scalar1=mix[:, cb : cb + 1],
+                scalar2=None, op0=ALU.mult,
+            )
             nc.vector.scalar_tensor_tensor(
                 out=planes[:, cb, :], in0=xt[:], scalar=keep_share[:, cb : cb + 1],
                 in1=late[:, PAD - 1 : PAD - 1 + T], op0=ALU.mult, op1=ALU.add,
@@ -139,7 +142,7 @@ def tile_full_tmix_params_pc_t_kernel(tc, x, x_w, w0, w1, w2, out):
                         in0=planes[:, PACK * g : PACK * (g + 1), :].rearrange("p j t -> p t j"),
                         scalar1=1.0, scalar2=0.0, op0=ALU.mult, op1=ALU.add,
                     )
-                elif b > 0:
+                else:
                     for tg in range(T_GROUPS):
                         pack(b, tg)
 
@@ -156,11 +159,67 @@ def tile_full_tmix_params_pc_t_kernel(tc, x, x_w, w0, w1, w2, out):
                     in_=grouped[:, g, tokens, :].rearrange("p c j -> p (c j)"),
                 )
 
+        head_banks = {}
+
+        def head_transpose(u):
+            tg, pair = divmod(u, C_BLOCKS // 2)
+            head_banks[u] = psum_x.tile([P, 2, T_GROUP], BF16, name="xt", tag="xt")
+            for i in range(2):
+                cb = 2 * pair + i
+                for t in range(T_GROUP // P):
+                    nc.tensor.transpose(
+                        out=head_banks[u][:, i, P * t : P * (t + 1)],
+                        in_=x_tiles[0][:, (T_GROUP // P) * tg + t, P * cb : P * (cb + 1)],
+                        identity=ident_bf[:],
+                    )
+
+        def head_scale(u):
+            tg, pair = divmod(u, C_BLOCKS // 2)
+            for i in range(2):
+                cb = 2 * pair + i
+                nc.scalar.activation(
+                    out=carried[:, cb, PAD + T_GROUP * tg : PAD + T_GROUP * (tg + 1)],
+                    in_=head_banks[u][:, i, :], func=ACT.Copy, scale=mix[:, cb : cb + 1],
+                )
+
+        def head_mix(u):
+            tg, pair = divmod(u, C_BLOCKS // 2)
+            for i in range(2):
+                cb = 2 * pair + i
+                nc.vector.scalar_tensor_tensor(
+                    out=planes[:, cb, T_GROUP * tg : T_GROUP * (tg + 1)],
+                    in0=head_banks[u][:, i, :], scalar=keep_share[:, cb : cb + 1],
+                    in1=carried[:, cb, PAD - 1 + T_GROUP * tg : PAD - 1 + T_GROUP * (tg + 1)],
+                    op0=ALU.mult, op1=ALU.add,
+                )
+
+        def head_regroup(engine, tg, g):
+            tokens = slice(T_GROUP * tg, T_GROUP * (tg + 1))
+            source = planes[:, PACK * g : PACK * (g + 1), tokens]
+            if engine == "v":
+                nc.vector.tensor_copy(
+                    out=grouped[:, g, tokens, :].rearrange("p (c i) j -> p c j i", i=4),
+                    in_=source.rearrange("p j (c i) -> p c j i", i=4),
+                )
+            else:
+                nc.gpsimd.tensor_scalar(
+                    out=grouped[:, g, tokens, :], in0=source.rearrange("p j t -> p t j"),
+                    scalar1=1.0, scalar2=0.0, op0=ALU.mult, op1=ALU.add,
+                )
+
+        def head_quantise(tg):
+            tokens = slice(T_GROUP * tg, T_GROUP * (tg + 1))
+            for g in range(K1_PASSES):
+                nc.vector.quantize_mx(
+                    out=xw_codes[0][:, g, tokens].bitcast(FP8X4),
+                    scales=xw_scales[0][:, g, tokens],
+                    in_=grouped[:, g, tokens, :].rearrange("p c j -> p (c j)"),
+                )
+
         h_grouped = {}
         h_codes = {}
         h_scales = {}
         gate = keep.tile([P, C_BLOCKS, T], F32, name="gate")
-        table_warm = keep.tile([P, 1], F32, name="table_warm")
 
         def hidden(b, t):
             tg, i = divmod(t, T_GROUP // P)
@@ -232,32 +291,61 @@ def tile_full_tmix_params_pc_t_kernel(tc, x, x_w, w0, w1, w2, out):
                 )
             nc.sync.dma_start(out=out[b, P * t : P * (t + 1), :], in_=result[:])
 
-        for q in range(LEAD):
-            transpose_block(q)
-        for q in range(C_BLOCKS):
-            transpose_block(q + LEAD)
-            mix_block(q)
-        pack(0, 0)
+        xw_codes[0] = codes_pool.tile(
+            [P, K1_PASSES, T], U32, name="xw_codes", tag="xw_codes", align_bytes=64
+        )
+        xw_scales[0] = codes_pool.tile(
+            [P, K1_PASSES, T], U8, name="xw_scales", tag="xw_scales", align_bytes=64
+        )
+        w1_rows = w1_raw[:].rearrange("p (g j) n -> p g n j", j=PACK)
+        w2_rows = w2_raw[:].rearrange("p j c -> p c j")
+        half = C_BLOCKS // 2
+        for u in range(half):
+            head_transpose(u)
+        for u in range(half):
+            head_scale(u)
+        nc.gpsimd.tensor_scalar(
+            out=w1_grouped[:, 1], in0=w1_rows[:, 1], scalar1=1.0, scalar2=0.0,
+            op0=ALU.mult, op1=ALU.add,
+        )
+        nc.scalar.copy(out=w1_grouped[:, 0], in_=w1_rows[:, 0])
+        for u in range(half):
+            head_mix(u)
+            head_transpose(half + u)
         for g in range(K1_PASSES):
-            nc.scalar.copy(
-                out=w1_grouped[:, g],
-                in_=w1_raw[:, PACK * g : PACK * (g + 1), :].rearrange("p j n -> p n j"),
-            )
+            head_regroup("v", 0, g)
+        head_quantise(0)
+        for g in range(K1_PASSES):
             nc.vector.quantize_mx(
                 out=w1_codes[:, g, :].bitcast(FP8X4),
                 scales=w1_scales[:, g, :],
                 in_=w1_grouped[:, g].rearrange("p n j -> p (n j)"),
             )
-        pack(0, 1)
+        head_scale(half)
+        head_scale(half + 1)
+        nc.scalar.copy(out=w2_grouped[:, 0 : C // 2], in_=w2_rows[:, 0 : C // 2])
         nc.vector.tensor_copy(
-            out=w2_grouped[:].rearrange("p (c i) j -> p c j i", i=4),
-            in_=w2_raw[:].rearrange("p j (c i) -> p c j i", i=4),
+            out=w2_grouped[:, C // 2 :].rearrange("p (c i) j -> p c j i", i=4),
+            in_=w2_raw[:, :, C // 2 :].rearrange("p j (c i) -> p c j i", i=4),
         )
-        nc.vector.quantize_mx(
-            out=w2_codes[:].bitcast(FP8X4),
-            scales=w2_scales[:],
-            in_=w2_grouped[:].rearrange("p c j -> p (c j)"),
-        )
+        head_mix(half)
+        head_mix(half + 1)
+        head_regroup("v", 1, 0)
+
+        def second_chunk():
+            nc.vector.quantize_mx(
+                out=w2_codes[:].bitcast(FP8X4),
+                scales=w2_scales[:],
+                in_=w2_grouped[:].rearrange("p c j -> p (c j)"),
+            )
+            quantise_hidden(0)
+            for u in (half + 2, half + 3):
+                head_scale(u)
+            for u in (half + 2, half + 3):
+                head_mix(u)
+            head_regroup("v", 1, 1)
+            head_quantise(1)
+            transpose_block(C_BLOCKS)
 
         def mix_behind(b, bank):
             if bank % BANKS_A_BLOCK == BANKS_A_BLOCK - 1:
@@ -265,21 +353,47 @@ def tile_full_tmix_params_pc_t_kernel(tc, x, x_w, w0, w1, w2, out):
                 transpose_block(q)
                 mix_block(q - LEAD if b == 0 else q)
 
+        placed = [0]
+
+        def place(count):
+            for q in range(C_BLOCKS + placed[0], C_BLOCKS + placed[0] + count):
+                transpose_block(q + LEAD)
+                mix_block(q)
+            placed[0] += count
+
         for b in range(B):
             if b + 2 < B:
                 load_x(b + 2)
+            if b == 0:
+                for tg in range(T_GROUPS):
+                    for i in range(T_GROUP // P):
+                        hidden(b, (T_GROUP // P) * tg + i)
+                        if tg == 1 and i in TANH_PLACES:
+                            place(1)
+                    if tg == 0:
+                        second_chunk()
+                    else:
+                        quantise_hidden(1)
+                    for cs in range(C_BLOCKS):
+                        gates(tg, cs)
+                        if tg == 1 and cs in GATE_PLACES:
+                            place(1)
+                for t in range(T_TILES):
+                    output(b, t)
+                    if t in OUT_PLACES:
+                        place(1)
+                continue
             nc.scalar.activation(out=table_warm[:], in_=columns[:, 0:1], func=ACT.Sigmoid)
             for t in range(T_TILES):
                 hidden(b, t)
                 if t % (T_GROUP // P) == T_GROUP // P - 1:
                     quantise_hidden(t // (T_GROUP // P))
+                    if b == 1 and t < T_TILES - 1:
+                        mix_block(2 * C_BLOCKS)
                 mix_behind(b, t)
             for tg in range(T_GROUPS):
                 for cs in range(C_BLOCKS):
                     gates(tg, cs)
                     mix_behind(b, T_TILES + C_BLOCKS * tg + cs)
-            if b == 0:
-                for q in range(2 * C_BLOCKS, 2 * C_BLOCKS + LEAD):
-                    mix_block(q)
             for t in range(T_TILES):
                 output(b, t)

@@ -16,20 +16,28 @@ PACK = 4
 B, T, C, DW = 4, 1024, 1024, 512
 C_BLOCKS = C // P
 K1_PASSES = C // (P * PACK)
-T_TILES = T // P
-T_GROUP = 512
-T_GROUPS = T // T_GROUP
+CHUNK = 512
+CHUNKS = T // CHUNK
+TILES = CHUNK // P
 BANK = 512
 PAD = 8
-X_PIECE = 2 * P
-RING = 8
-X_BANKS = 4
-TANH_PLACES = (1, 3)
-GATE_PLACES = (1, 3, 5, 7)
-OUT_PLACES = (0, 2)
-LEAD = 1
-SCALAR_BANKS = T_TILES + T_GROUPS * C_BLOCKS
-BANKS_A_BLOCK = SCALAR_BANKS // C_BLOCKS
+PAIR = 2
+PIECE = 512
+HEAD_UNITS = C_BLOCKS // 2
+FEED_PLACES = (("h", 0), ("h", 2), ("z", 1), ("z", 4))
+ROUNDS = ((0, 1), (2, 3, 4), (5, 6, 7))
+G_LAG = 0
+G_HALVES = (0, 1)
+Q_LAG = (2, 1)
+START = (("h", 0, 0), ("q", 0, 0), ("z", 0, 0), ("z", 0, 1), ("h", 1, 2), ("q", 1, 0), ("z", 1, 2), ("z", 1, 5))
+V_FROM = 8
+SPACING = 5.3
+LOAD = 4
+HELD = 0
+LIMIT = (34, 34, 34, 34)
+ROUND = 2
+T_AHEAD = 3
+C_AHEAD = 1
 
 FLOPS = 2 * B * T * (C * DW + DW * C)
 
@@ -39,47 +47,67 @@ def tile_full_tmix_params_pc_t_kernel(tc, x, x_w, w0, w1, w2, out):
     with tc.manual_schedule(), tc.tile_pool(name="keep", bufs=1) as keep, tc.tile_pool(
         name="xin", bufs=2
     ) as xin_pool, tc.tile_pool(name="codes", bufs=2) as codes_pool, tc.tile_pool(
+        name="gates", bufs=3
+    ) as gate_pool, tc.tile_pool(
         name="res", bufs=7
-    ) as res_pool, tc.psum_pool(name="psx", bufs=X_BANKS) as psum_x, tc.psum_pool(
+    ) as res_pool, tc.psum_pool(name="psx", bufs=4) as psum_x, tc.psum_pool(
         name="psa", bufs=4
     ) as psum_acc:
         table_warm = keep.tile([P, 1], F32, name="table_warm")
         nc.vector.memset(table_warm[:], 0.0)
         nc.scalar.activation(out=table_warm[:], in_=table_warm[:], func=ACT.Sigmoid)
-        vectors = keep.tile([P, P], BF16, name="vectors")
+
+        vectors = keep.tile([P, 3, P], BF16, name="vectors")
         nc.vector.memset(vectors[:], 0.0)
-        nc.sync.dma_start(out=vectors[0:C_BLOCKS, :], in_=x_w.rearrange("(r c) -> r c", c=P))
+        x_w_rows = vectors[:, 0:2, :].rearrange("p a c -> p (a c)")
+        w0_rows = vectors[:, 2, :]
         nc.sync.dma_start(
-            out=vectors[C_BLOCKS : 2 * C_BLOCKS, :], in_=w0.rearrange("(r c) -> r c", c=P)
+            out=x_w_rows[0 : C_BLOCKS // PAIR, :], in_=x_w.rearrange("(r c) -> r c", c=PAIR * P)
         )
+        nc.sync.dma_start(out=w0_rows[0:C_BLOCKS, :], in_=w0.rearrange("(r c) -> r c", c=P))
         x_tiles = {}
 
-        def load_x(b, t0=0, t1=T_TILES, piece=C // 2):
-            if t0 == 0:
-                x_tiles[b] = xin_pool.tile([P, T_TILES, C], BF16, name="x_sb", tag="x_sb")
+        def load_x(b, t0, n, pieces):
+            if b not in x_tiles:
+                x_tiles[b] = xin_pool.tile([P, T // P, C], BF16, name="x_sb", tag="x_sb")
             rows = x[b].rearrange("(t p) c -> p t c", p=P)
-            for c0 in range(0, C, piece):
+            width = C // pieces
+            for c0 in range(0, C, width):
                 nc.sync.dma_start(
-                    out=x_tiles[b][:, t0:t1, c0 : c0 + piece], in_=rows[:, t0:t1, c0 : c0 + piece]
+                    out=x_tiles[b][:, t0 // P : (t0 + n) // P, c0 : c0 + width],
+                    in_=rows[:, t0 // P : (t0 + n) // P, c0 : c0 + width],
                 )
 
-        load_x(0, 0, T_TILES // 2, X_PIECE)
-        w1_raw = keep.tile([P, K1_PASSES * PACK, DW], BF16, name="w1_raw")
-        nc.sync.dma_start(out=w1_raw[:], in_=w1.rearrange("(r p) n -> p r n", p=P))
-        load_x(0, T_TILES // 2, T_TILES)
-        w2_raw = keep.tile([P, PACK, C], BF16, name="w2_raw")
-        nc.sync.dma_start(out=w2_raw[:], in_=w2.rearrange("(j p) c -> p j c", p=P))
-        load_x(1)
+        stage_1 = gate_pool.tile([P, 2, PACK * C], BF16, name="stage_1", tag="gate", align_bytes=64)
+        stage_2 = gate_pool.tile([P, 2, PACK * C], BF16, name="stage_2", tag="gate", align_bytes=64)
+        w1_raw = stage_1[:, 0, :].rearrange("p (r n) -> p r n", n=DW)
+        w1_grouped = stage_1[:, 1, :].rearrange("p (g n) -> p g n", g=K1_PASSES)
+        w2_raw = stage_2[:, 0, :].rearrange("p (j c) -> p j c", c=C)
+        w2_grouped = stage_2[:, 1, :]
 
-        ident_bf = keep.tile([P, P], BF16, name="ident_bf")
-        make_identity(nc, ident_bf[:])
+        load_x(0, 0, CHUNK, 4)
+        nc.sync.dma_start(
+            out=w1_raw.rearrange("p (v e) n -> p v e n", e=PAIR),
+            in_=w1.rearrange("(v p e) n -> p v e n", p=P, e=PAIR),
+        )
+        load_x(0, CHUNK, CHUNK, 1)
+        nc.sync.dma_start(out=w2_raw, in_=w2.rearrange("(j p) c -> p j c", p=P))
+        load_x(1, 0, T, 2)
+
         ident_f32 = keep.tile([P, P], F32, name="ident_f32")
         make_identity(nc, ident_f32[:])
+        ident_bf = keep.tile([P, P], BF16, name="ident_bf")
+        make_identity(nc, ident_bf[:])
 
-        vectors_t = psum_acc.tile([P, P], BF16, name="vectors_t", tag="acc")
-        nc.tensor.transpose(out=vectors_t[:], in_=vectors[:], identity=ident_bf[:])
         columns = keep.tile([P, 2 * C_BLOCKS], F32, name="columns")
-        nc.vector.tensor_copy(out=columns[:], in_=vectors_t[:, 0 : 2 * C_BLOCKS])
+        x_w_t = psum_acc.tile([P, P], F32, name="x_w_t", tag="acc")
+        nc.tensor.transpose(out=x_w_t[:], in_=x_w_rows.bitcast(F32), identity=ident_f32[:])
+        nc.vector.tensor_copy(
+            out=columns[:, 0:C_BLOCKS], in_=x_w_t[:, 0 : C_BLOCKS // PAIR].bitcast(BF16)
+        )
+        w0_t = psum_acc.tile([P, P], BF16, name="w0_t", tag="acc")
+        nc.tensor.transpose(out=w0_t[:], in_=w0_rows, identity=ident_bf[:])
+        nc.vector.tensor_copy(out=columns[:, C_BLOCKS : 2 * C_BLOCKS], in_=w0_t[:, 0:C_BLOCKS])
         mix = columns[:, 0:C_BLOCKS]
         bias = columns[:, C_BLOCKS : 2 * C_BLOCKS]
         keep_share = keep.tile([P, C_BLOCKS], F32, name="keep_share")
@@ -87,148 +115,150 @@ def tile_full_tmix_params_pc_t_kernel(tc, x, x_w, w0, w1, w2, out):
             out=keep_share[:], in0=mix, scalar1=-1.0, scalar2=1.0, op0=ALU.mult, op1=ALU.add
         )
 
-        w1_grouped = keep.tile([P, K1_PASSES, DW, PACK], BF16, name="w1_grouped", align_bytes=64)
         w1_codes = keep.tile([P, K1_PASSES, DW], U32, name="w1_codes", align_bytes=64)
         w1_scales = keep.tile([P, K1_PASSES, DW], U8, name="w1_scales", align_bytes=64)
-        w2_grouped = keep.tile([P, C, PACK], BF16, name="w2_grouped", align_bytes=64)
         w2_codes = keep.tile([P, C], U32, name="w2_codes", align_bytes=64)
         w2_scales = keep.tile([P, C], U8, name="w2_scales", align_bytes=64)
 
-        carried = keep.tile([P, RING, PAD + T], F32, name="carried")
-        nc.vector.memset(carried[:, :, 0:PAD], 0.0)
+        carried = keep.tile([P, C_BLOCKS // PAIR, PAIR * (PAD + T)], F32, name="carried")
+        by_channel = carried[:].rearrange("p v (e t) -> p (v e) t", e=PAIR)
+        by_token = carried[:].rearrange("p v (t e) -> p v t e", e=PAIR)
+        nc.vector.memset(by_channel[:, :, 0:PAD], 0.0)
         planes = keep.tile([P, C_BLOCKS, T], BF16, name="planes")
         grouped = keep.tile([P, K1_PASSES, T, PACK], BF16, name="grouped", align_bytes=64)
-        xt_tiles = {}
+
+        units = []
+        for b in range(B):
+            for t0 in range(0, T, CHUNK):
+                for cb in range(0, C_BLOCKS, 2):
+                    units.append((b, t0, CHUNK, cb, 2))
+        scalar_lates = [u for u in range(4 * HEAD_UNITS) if u < HEAD_UNITS or u < 8]
+        banks = {}
         xw_codes = {}
         xw_scales = {}
+        later = []
 
-        def transpose_block(q):
-            b, cb = divmod(q, C_BLOCKS)
-            if b >= B:
+        def transpose_unit(u):
+            if u >= len(units):
                 return
-            xt_tiles[q] = psum_x.tile([P, T], BF16, name="xt", tag="xt")
-            for t in range(T_TILES):
+            b, t0, n, cb, k = units[u]
+            banks[u] = psum_x.tile([P, n], F32, name="xt", tag="xt")
+            for t in range(n // P):
                 nc.tensor.transpose(
-                    out=xt_tiles[q][:, P * t : P * (t + 1)],
-                    in_=x_tiles[b][:, t, P * cb : P * (cb + 1)],
-                    identity=ident_bf[:],
+                    out=banks[u][:, P * t : P * (t + 1)],
+                    in_=x_tiles[b][:, t0 // P + t, P * cb : P * (cb + PAIR)].bitcast(F32),
+                    identity=ident_f32[:],
                 )
 
-        def mix_block(q):
-            b, cb = divmod(q, C_BLOCKS)
-            if b >= B:
+        def pairs(u):
+            return banks[u][:].bitcast(BF16).rearrange("p (t e) -> p t e", e=PAIR)
+
+        def scale_unit(u):
+            if u >= len(units):
                 return
-            xt = xt_tiles[q]
-            late = carried[:, q % RING, :]
-            nc.vector.tensor_scalar(
-                out=late[:, PAD : PAD + T], in0=xt[:], scalar1=mix[:, cb : cb + 1],
-                scalar2=None, op0=ALU.mult,
+            b, t0, n, cb, k = units[u]
+            if u in scalar_lates:
+                for e in range(PAIR):
+                    nc.scalar.activation(
+                        out=by_channel[:, cb + e, PAD + t0 : PAD + t0 + n],
+                        in_=pairs(u)[:, :, e], func=ACT.Copy, scale=mix[:, cb + e : cb + e + 1],
+                    )
+                return
+            if b == 1 and t0 == 0:
+                nc.vector.memset(by_token[:, cb // PAIR, PAD - 1 : PAD, :], 0.0)
+            nc.vector.tensor_tensor(
+                out=by_token[:, cb // PAIR, PAD + t0 : PAD + t0 + n, :], in0=pairs(u),
+                in1=mix[:, cb : cb + PAIR].unsqueeze(1).to_broadcast([P, n, PAIR]), op=ALU.mult,
             )
-            nc.vector.scalar_tensor_tensor(
-                out=planes[:, cb, :], in0=xt[:], scalar=keep_share[:, cb : cb + 1],
-                in1=late[:, PAD - 1 : PAD - 1 + T], op0=ALU.mult, op1=ALU.add,
-            )
-            if cb % PACK == PACK - 1:
-                g = cb // PACK
-                if g == 0:
-                    xw_codes[b] = codes_pool.tile(
-                        [P, K1_PASSES, T], U32, name="xw_codes", tag="xw_codes", align_bytes=64
-                    )
-                    xw_scales[b] = codes_pool.tile(
-                        [P, K1_PASSES, T], U8, name="xw_scales", tag="xw_scales", align_bytes=64
-                    )
-                    nc.gpsimd.tensor_scalar(
-                        out=grouped[:, g],
-                        in0=planes[:, PACK * g : PACK * (g + 1), :].rearrange("p j t -> p t j"),
-                        scalar1=1.0, scalar2=0.0, op0=ALU.mult, op1=ALU.add,
-                    )
-                else:
-                    for tg in range(T_GROUPS):
-                        pack(b, tg)
 
-        def pack(b, tg):
-            tokens = slice(T_GROUP * tg, T_GROUP * (tg + 1))
-            nc.vector.tensor_copy(
-                out=grouped[:, 1, tokens, :].rearrange("p (c i) j -> p c j i", i=4),
-                in_=planes[:, PACK : 2 * PACK, tokens].rearrange("p j (c i) -> p c j i", i=4),
-            )
-            for g in range(K1_PASSES):
-                nc.vector.quantize_mx(
-                    out=xw_codes[b][:, g, tokens].bitcast(FP8X4),
-                    scales=xw_scales[b][:, g, tokens],
-                    in_=grouped[:, g, tokens, :].rearrange("p c j -> p (c j)"),
-                )
-
-        head_banks = {}
-
-        def head_transpose(u):
-            tg, pair = divmod(u, C_BLOCKS // 2)
-            head_banks[u] = psum_x.tile([P, 2, T_GROUP], BF16, name="xt", tag="xt")
-            for i in range(2):
-                cb = 2 * pair + i
-                for t in range(T_GROUP // P):
-                    nc.tensor.transpose(
-                        out=head_banks[u][:, i, P * t : P * (t + 1)],
-                        in_=x_tiles[0][:, (T_GROUP // P) * tg + t, P * cb : P * (cb + 1)],
-                        identity=ident_bf[:],
-                    )
-
-        def head_scale(u):
-            tg, pair = divmod(u, C_BLOCKS // 2)
-            for i in range(2):
-                cb = 2 * pair + i
-                nc.scalar.activation(
-                    out=carried[:, cb, PAD + T_GROUP * tg : PAD + T_GROUP * (tg + 1)],
-                    in_=head_banks[u][:, i, :], func=ACT.Copy, scale=mix[:, cb : cb + 1],
-                )
-
-        def head_mix(u):
-            tg, pair = divmod(u, C_BLOCKS // 2)
-            for i in range(2):
-                cb = 2 * pair + i
+        def mix_unit(u):
+            b, t0, n, cb, k = units[u]
+            for e in range(PAIR):
+                earlier = slice(PAD - 1 + t0, PAD - 1 + t0 + n)
                 nc.vector.scalar_tensor_tensor(
-                    out=planes[:, cb, T_GROUP * tg : T_GROUP * (tg + 1)],
-                    in0=head_banks[u][:, i, :], scalar=keep_share[:, cb : cb + 1],
-                    in1=carried[:, cb, PAD - 1 + T_GROUP * tg : PAD - 1 + T_GROUP * (tg + 1)],
+                    out=planes[:, cb + e, t0 : t0 + n], in0=pairs(u)[:, :, e],
+                    scalar=keep_share[:, cb + e : cb + e + 1],
+                    in1=by_channel[:, cb + e, earlier] if b == 0
+                    else by_token[:, cb // PAIR, earlier, e],
                     op0=ALU.mult, op1=ALU.add,
                 )
-
-        def head_regroup(engine, tg, g):
-            tokens = slice(T_GROUP * tg, T_GROUP * (tg + 1))
-            source = planes[:, PACK * g : PACK * (g + 1), tokens]
-            if engine == "v":
-                nc.vector.tensor_copy(
-                    out=grouped[:, g, tokens, :].rearrange("p (c i) j -> p c j i", i=4),
-                    in_=source.rearrange("p j (c i) -> p c j i", i=4),
+            if (cb + k) % PACK == 0:
+                g = cb // PACK
+                for p0 in range(t0, t0 + n, PIECE):
+                    later.append((u + G_LAG if u >= HEAD_UNITS else HEAD_UNITS - 1, regroup, b, g, slice(p0, p0 + PIECE), u >= HEAD_UNITS and (g == 0 or 2 * HEAD_UNITS <= u < V_FROM and g in G_HALVES)))
+                    later.append((u + (Q_LAG[g] if 2 * HEAD_UNITS <= u < V_FROM else (2, 0)[g]) if u >= HEAD_UNITS else HEAD_UNITS - 1, quantise_x, b, g, slice(p0, p0 + PIECE), False))
+            if cb == 0 and t0 == 0:
+                xw_codes[b] = codes_pool.tile(
+                    [P, K1_PASSES, T], U32, name="xw_codes", tag="xw_codes", align_bytes=64
                 )
-            else:
+                xw_scales[b] = codes_pool.tile(
+                    [P, K1_PASSES, T], U8, name="xw_scales", tag="xw_scales", align_bytes=64
+                )
+
+        def regroup(b, g, tokens, on_gpsimd):
+            if on_gpsimd:
                 nc.gpsimd.tensor_scalar(
-                    out=grouped[:, g, tokens, :], in0=source.rearrange("p j t -> p t j"),
+                    out=grouped[:, g, tokens, :],
+                    in0=planes[:, PACK * g : PACK * (g + 1), tokens].rearrange("p j t -> p t j"),
                     scalar1=1.0, scalar2=0.0, op0=ALU.mult, op1=ALU.add,
                 )
-
-        def head_quantise(tg):
-            tokens = slice(T_GROUP * tg, T_GROUP * (tg + 1))
-            for g in range(K1_PASSES):
-                nc.vector.quantize_mx(
-                    out=xw_codes[0][:, g, tokens].bitcast(FP8X4),
-                    scales=xw_scales[0][:, g, tokens],
-                    in_=grouped[:, g, tokens, :].rearrange("p c j -> p (c j)"),
+            else:
+                nc.vector.tensor_copy(
+                    out=grouped[:, g, tokens, :].rearrange("p (c i) j -> p c j i", i=4),
+                    in_=planes[:, PACK * g : PACK * (g + 1), tokens].rearrange(
+                        "p j (c i) -> p c j i", i=4
+                    ),
                 )
+
+        def quantise_x(b, g, tokens, unused):
+            nc.vector.quantize_mx(
+                out=xw_codes[b][:, g, tokens].bitcast(FP8X4),
+                scales=xw_scales[b][:, g, tokens],
+                in_=grouped[:, g, tokens, :].rearrange("p c j -> p (c j)"),
+            )
+
+        def run_later(u):
+            due = [item for item in later if item[0] <= u]
+            for item in [i for i in due if i[1] is regroup] + [i for i in due if i[1] is not regroup]:
+                later.remove(item)
+                item[1](*item[2:])
+
+        def finish_chunk(b, c):
+            chunk = slice(CHUNK * c, CHUNK * (c + 1))
+            due = [item for item in later if item[2] == b and item[4] == chunk]
+            for item in [i for i in due if i[1] is regroup] + [i for i in due if i[1] is not regroup]:
+                later.remove(item)
+                item[1](*item[2:])
+
+        step = [0]
+        last_units = [(CHUNK, CHUNK, C_BLOCKS - 2, 2)]
+
+        def advance():
+            u = step[0]
+            step[0] = u + 1
+            if u < len(units):
+                if u > HEAD_UNITS:
+                    transpose_unit(u + T_AHEAD)
+                if u + T_AHEAD < len(units) and units[u + T_AHEAD][1:] in last_units:
+                    b = units[u + T_AHEAD][0] + 2
+                    if b < B:
+                        load_x(b, 0, T, 2)
+                scale_unit(u + C_AHEAD)
+                mix_unit(u)
+            run_later(u)
 
         h_grouped = {}
         h_codes = {}
         h_scales = {}
-        gate = keep.tile([P, C_BLOCKS, T], F32, name="gate")
+        gate = {}
 
-        def hidden(b, t):
-            tg, i = divmod(t, T_GROUP // P)
+        def hidden(b, c, i):
             if i == 0:
-                h_grouped[tg] = codes_pool.tile(
-                    [P, T_GROUP, PACK], BF16, name="h_grouped", tag="h_grouped", align_bytes=64
+                h_grouped[c] = codes_pool.tile(
+                    [P, CHUNK, PACK], BF16, name="h_grouped", tag="h_grouped", align_bytes=64
                 )
             acc = psum_acc.tile([P, PACK, P], F32, name="h_acc", tag="acc")
-            tokens = slice(P * t, P * (t + 1))
+            tokens = slice(CHUNK * c + P * i, CHUNK * c + P * (i + 1))
             for m in range(PACK):
                 for g in range(K1_PASSES):
                     nc.tensor.matmul_mx(
@@ -241,159 +271,152 @@ def tile_full_tmix_params_pc_t_kernel(tc, x, x_w, w0, w1, w2, out):
                         stop=(g == K1_PASSES - 1),
                     )
             nc.scalar.activation(
-                out=h_grouped[tg][:, P * i : P * (i + 1), :],
+                out=h_grouped[c][:, P * i : P * (i + 1), :],
                 in_=acc[:].rearrange("p m t -> p t m"),
                 func=ACT.Tanh,
             )
 
-        def quantise_hidden(tg):
-            h_codes[tg] = codes_pool.tile(
-                [P, T_GROUP], U32, name="h_codes", tag="h_codes", align_bytes=64
+        def quantise_hidden(c):
+            h_codes[c] = codes_pool.tile(
+                [P, CHUNK], U32, name="h_codes", tag="h_codes", align_bytes=64
             )
-            h_scales[tg] = codes_pool.tile(
-                [P, T_GROUP], U8, name="h_scales", tag="h_scales", align_bytes=64
+            h_scales[c] = codes_pool.tile(
+                [P, CHUNK], U8, name="h_scales", tag="h_scales", align_bytes=64
             )
             nc.vector.quantize_mx(
-                out=h_codes[tg][:].bitcast(FP8X4),
-                scales=h_scales[tg][:],
-                in_=h_grouped[tg][:].rearrange("p t j -> p (t j)"),
+                out=h_codes[c][:].bitcast(FP8X4),
+                scales=h_scales[c][:],
+                in_=h_grouped[c][:].rearrange("p t j -> p (t j)"),
             )
 
-        def gates(tg, cs):
-            acc = psum_acc.tile([P, T_GROUP], F32, name="z_acc", tag="acc")
+        def gates(b, c, cs):
+            if cs == 0:
+                gate[b, c] = gate_pool.tile(
+                    [P, C_BLOCKS, CHUNK], F32, name="gate", tag="gate", align_bytes=64
+                )
+            acc = psum_acc.tile([P, CHUNK], F32, name="z_acc", tag="acc")
             nc.tensor.matmul_mx(
                 out=acc[:],
                 lhsT=w2_codes[:, P * cs : P * (cs + 1)].bitcast(FP8X4),
                 lhsT_scale=w2_scales[:, P * cs : P * (cs + 1)],
-                rhs=h_codes[tg][:].bitcast(FP8X4),
-                rhs_scale=h_scales[tg][:],
+                rhs=h_codes[c][:].bitcast(FP8X4),
+                rhs_scale=h_scales[c][:],
                 start=True,
                 stop=True,
             )
             nc.scalar.activation(
-                out=gate[:, cs, T_GROUP * tg : T_GROUP * (tg + 1)], in_=acc[:], func=ACT.Sigmoid,
+                out=gate[b, c][:, cs, :], in_=acc[:], func=ACT.Sigmoid,
                 bias=bias[:, cs : cs + 1], scale=1.0,
             )
 
-        def output(b, t):
-            result = res_pool.tile([P, C], F32, name="result", tag="result")
-            for half in range(C // BANK):
-                acc = psum_acc.tile([P, BANK], F32, name="o_acc", tag="acc")
-                for i in range(BANK // P):
-                    nc.tensor.transpose(
-                        out=acc[:, P * i : P * (i + 1)],
-                        in_=gate[:, (BANK // P) * half + i, P * t : P * (t + 1)],
-                        identity=ident_f32[:],
-                    )
-                nc.scalar.activation(
-                    out=result[:, BANK * half : BANK * (half + 1)], in_=acc[:], func=ACT.Ln,
-                    scale=math.exp(-0.5),
-                )
-            nc.sync.dma_start(out=out[b, P * t : P * (t + 1), :], in_=result[:])
+        results = {}
 
-        xw_codes[0] = codes_pool.tile(
-            [P, K1_PASSES, T], U32, name="xw_codes", tag="xw_codes", align_bytes=64
-        )
-        xw_scales[0] = codes_pool.tile(
-            [P, K1_PASSES, T], U8, name="xw_scales", tag="xw_scales", align_bytes=64
-        )
-        w1_rows = w1_raw[:].rearrange("p (g j) n -> p g n j", j=PACK)
-        w2_rows = w2_raw[:].rearrange("p j c -> p c j")
-        half = C_BLOCKS // 2
-        for u in range(half):
-            head_transpose(u)
-        for u in range(half):
-            head_scale(u)
+        def output(b, c, i, half):
+            t = TILES * c + i
+            if half == 0:
+                results[0] = res_pool.tile([P, C], F32, name="result", tag="result")
+            acc = psum_acc.tile([P, BANK], F32, name="o_acc", tag="acc")
+            for k in range(BANK // P):
+                nc.tensor.transpose(
+                    out=acc[:, P * k : P * (k + 1)],
+                    in_=gate[b, c][:, (BANK // P) * half + k, P * i : P * (i + 1)],
+                    identity=ident_f32[:],
+                )
+            nc.scalar.activation(
+                out=results[0][:, BANK * half : BANK * (half + 1)], in_=acc[:], func=ACT.Ln,
+                scale=math.exp(-0.5),
+            )
+            if half == 1:
+                nc.sync.dma_start(out=out[b, P * t : P * (t + 1), :], in_=results[0][:])
+
+        w1_rows = w1_raw.rearrange("p (g j) n -> p g n j", j=PACK)
+        w1_cols = w1_grouped.rearrange("p g (n j) -> p g n j", j=PACK)
+        for u in range(HEAD_UNITS):
+            transpose_unit(u)
+        for u in range(HEAD_UNITS):
+            scale_unit(u)
         nc.gpsimd.tensor_scalar(
-            out=w1_grouped[:, 1], in0=w1_rows[:, 1], scalar1=1.0, scalar2=0.0,
-            op0=ALU.mult, op1=ALU.add,
+            out=w1_cols[:, 1], in0=w1_rows[:, 1], scalar1=1.0, scalar2=0.0, op0=ALU.mult, op1=ALU.add
         )
-        nc.scalar.copy(out=w1_grouped[:, 0], in_=w1_rows[:, 0])
-        for u in range(half):
-            head_mix(u)
-            head_transpose(half + u)
-        for g in range(K1_PASSES):
-            head_regroup("v", 0, g)
-        head_quantise(0)
+        nc.scalar.copy(out=w1_cols[:, 0], in_=w1_rows[:, 0])
+        for u in range(HEAD_UNITS):
+            mix_unit(u)
+            run_later(u)
+            transpose_unit(u + HEAD_UNITS)
+        step[0] = HEAD_UNITS
         for g in range(K1_PASSES):
             nc.vector.quantize_mx(
                 out=w1_codes[:, g, :].bitcast(FP8X4),
                 scales=w1_scales[:, g, :],
-                in_=w1_grouped[:, g].rearrange("p n j -> p (n j)"),
+                in_=w1_grouped[:, g, :],
             )
-        head_scale(half)
-        head_scale(half + 1)
-        nc.scalar.copy(out=w2_grouped[:, 0 : C // 2], in_=w2_rows[:, 0 : C // 2])
+        w2_rows = w2_raw.rearrange("p j c -> p c j")
+        w2_cols = w2_grouped.rearrange("p (c j) -> p c j", j=PACK)
+        nc.scalar.copy(out=w2_cols[:, 0 : C // 2], in_=w2_rows[:, 0 : C // 2])
         nc.vector.tensor_copy(
-            out=w2_grouped[:, C // 2 :].rearrange("p (c i) j -> p c j i", i=4),
+            out=w2_cols[:, C // 2 :].rearrange("p (c i) j -> p c j i", i=4),
             in_=w2_raw[:, :, C // 2 :].rearrange("p j (c i) -> p c j i", i=4),
         )
-        head_mix(half)
-        head_mix(half + 1)
-        head_regroup("v", 1, 0)
+        for u in range(C_AHEAD):
+            scale_unit(HEAD_UNITS + u)
 
-        def second_chunk():
+        def quantise_w2():
             nc.vector.quantize_mx(
-                out=w2_codes[:].bitcast(FP8X4),
-                scales=w2_scales[:],
-                in_=w2_grouped[:].rearrange("p c j -> p (c j)"),
+                out=w2_codes[:].bitcast(FP8X4), scales=w2_scales[:], in_=w2_grouped
             )
-            quantise_hidden(0)
-            for u in (half + 2, half + 3):
-                head_scale(u)
-            for u in (half + 2, half + 3):
-                head_mix(u)
-            head_regroup("v", 1, 1)
-            head_quantise(1)
-            transpose_block(C_BLOCKS)
 
-        def mix_behind(b, bank):
-            if bank % BANKS_A_BLOCK == BANKS_A_BLOCK - 1:
-                q = C_BLOCKS * (b + 1) + LEAD + bank // BANKS_A_BLOCK
-                transpose_block(q)
-                mix_block(q - LEAD if b == 0 else q)
+        slots = [0]
 
-        placed = [0]
+        credit = [0.0]
 
-        def place(count):
-            for q in range(C_BLOCKS + placed[0], C_BLOCKS + placed[0] + count):
-                transpose_block(q + LEAD)
-                mix_block(q)
-            placed[0] += count
+        def feed(slots_passed):
+            credit[0] += slots_passed
+            while credit[0] >= SPACING and step[0] < len(units) + 2:
+                credit[0] -= SPACING
+                advance()
 
-        for b in range(B):
-            if b + 2 < B:
-                load_x(b + 2)
-            if b == 0:
-                for tg in range(T_GROUPS):
-                    for i in range(T_GROUP // P):
-                        hidden(b, (T_GROUP // P) * tg + i)
-                        if tg == 1 and i in TANH_PLACES:
-                            place(1)
-                    if tg == 0:
-                        second_chunk()
-                    else:
-                        quantise_hidden(1)
-                    for cs in range(C_BLOCKS):
-                        gates(tg, cs)
-                        if tg == 1 and cs in GATE_PLACES:
-                            place(1)
-                for t in range(T_TILES):
-                    output(b, t)
-                    if t in OUT_PLACES:
-                        place(1)
-                continue
-            nc.scalar.activation(out=table_warm[:], in_=columns[:, 0:1], func=ACT.Sigmoid)
-            for t in range(T_TILES):
-                hidden(b, t)
-                if t % (T_GROUP // P) == T_GROUP // P - 1:
-                    quantise_hidden(t // (T_GROUP // P))
-                    if b == 1 and t < T_TILES - 1:
-                        mix_block(2 * C_BLOCKS)
-                mix_behind(b, t)
-            for tg in range(T_GROUPS):
-                for cs in range(C_BLOCKS):
-                    gates(tg, cs)
-                    mix_behind(b, T_TILES + C_BLOCKS * tg + cs)
-            for t in range(T_TILES):
-                output(b, t)
+        def stage_order(r):
+            chunks = [divmod(k, CHUNKS) for k in ROUNDS[r]]
+            tanh = [[("h", bc, i) for i in range(TILES)] + [("q", bc, 0)] for bc in chunks]
+            sigmoid = [[("z", bc, cs) for cs in range(C_BLOCKS)] for bc in chunks]
+            if r == 0:
+                return tanh[0] + sigmoid[0] + tanh[1] + sigmoid[1]
+            order = tanh[0] + tanh[1]
+            for k in range(len(chunks)):
+                if k == 0:
+                    order += sigmoid[0]
+                elif k + 1 < len(chunks):
+                    order += sigmoid[k][: C_BLOCKS - HELD] + tanh[k + 1] + sigmoid[k][C_BLOCKS - HELD :]
+                else:
+                    order += sigmoid[k]
+            return order
+
+        for r, bs in enumerate(ROUNDS):
+            if r > 0:
+                feed(LOAD)
+                nc.scalar.activation(out=table_warm[:], in_=columns[:, 0:1], func=ACT.Sigmoid)
+            for kind, (b, c), i in stage_order(r):
+                if b == 0:
+                    if (kind, c, i) in START:
+                        advance()
+                elif kind != "q":
+                    feed(1)
+                if kind == "h":
+                    if i == 0:
+                        while not any(x[0] == b and x[1] + x[2] >= CHUNK * (c + 1) and x[3] + x[4] == C_BLOCKS for x in units[: step[0]]):
+                            advance()
+                        finish_chunk(b, c)
+                    hidden(b, c, i)
+                elif kind == "q":
+                    if r == 0 and c == 0:
+                        quantise_w2()
+                    quantise_hidden(c)
+                else:
+                    gates(b, c, i)
+            feed(LOAD)
+            for k in bs:
+                b, c = divmod(k, CHUNKS)
+                for i in range(TILES):
+                    for half in range(2):
+                        feed(1)
+                        output(b, c, i, half)

@@ -21,6 +21,7 @@ CHUNKS = T // CHUNK
 TILES = CHUNK // P
 BANK = 512
 PAD = 8
+HEAD_NAMES = ("x_0", "x_1", "x_2", "x_3")
 PAIR = 2
 PIECE = 512
 HEAD_UNITS = C_BLOCKS // 2
@@ -33,7 +34,7 @@ START = (("h", 0, 0), ("q", 0, 0), ("z", 0, 0), ("z", 0, 1), ("h", 1, 2), ("q", 
 V_FROM = 8
 SPACING = 5.3
 LOAD = 4
-HELD = 0
+HELD = 3
 LIMIT = (34, 34, 34, 34)
 ROUND = 2
 T_AHEAD = 3
@@ -45,7 +46,7 @@ FLOPS = 2 * B * T * (C * DW + DW * C)
 def tile_full_tmix_params_pc_t_kernel(tc, x, x_w, w0, w1, w2, out):
     nc = tc.nc
     with tc.manual_schedule(), tc.tile_pool(name="keep", bufs=1) as keep, tc.tile_pool(
-        name="xin", bufs=2
+        name="xin", bufs=4
     ) as xin_pool, tc.tile_pool(name="codes", bufs=2) as codes_pool, tc.tile_pool(
         name="gates", bufs=3
     ) as gate_pool, tc.tile_pool(
@@ -67,16 +68,19 @@ def tile_full_tmix_params_pc_t_kernel(tc, x, x_w, w0, w1, w2, out):
         nc.sync.dma_start(out=w0_rows[0:C_BLOCKS, :], in_=w0.rearrange("(r c) -> r c", c=P))
         x_tiles = {}
 
-        def load_x(b, t0, n, pieces):
-            if b not in x_tiles:
-                x_tiles[b] = xin_pool.tile([P, T // P, C], BF16, name="x_sb", tag="x_sb")
-            rows = x[b].rearrange("(t p) c -> p t c", p=P)
-            width = C // pieces
+        def load_x(k):
+            b, c = divmod(k, CHUNKS)
+            rows = x[b, CHUNK * c : CHUNK * (c + 1), :].rearrange("(t p) c -> p t c", p=P)
+            width = PAIR * P if k == 0 else C
             for c0 in range(0, C, width):
-                nc.sync.dma_start(
-                    out=x_tiles[b][:, t0 // P : (t0 + n) // P, c0 : c0 + width],
-                    in_=rows[:, t0 // P : (t0 + n) // P, c0 : c0 + width],
-                )
+                pool = keep if k == 0 else xin_pool
+                name = HEAD_NAMES[c0 // width] if k == 0 else "x_sb"
+                tile = pool.tile([P, TILES, width], BF16, name=name, tag=name)
+                nc.sync.dma_start(out=tile[:], in_=rows[:, :, c0 : c0 + width])
+                for v in range(width // (PAIR * P)):
+                    x_tiles[k, (c0 + v * PAIR * P) // (PAIR * P)] = tile[
+                        :, :, PAIR * P * v : PAIR * P * (v + 1)
+                    ]
 
         stage_1 = gate_pool.tile([P, 2, PACK * C], BF16, name="stage_1", tag="gate", align_bytes=64)
         stage_2 = gate_pool.tile([P, 2, PACK * C], BF16, name="stage_2", tag="gate", align_bytes=64)
@@ -85,14 +89,16 @@ def tile_full_tmix_params_pc_t_kernel(tc, x, x_w, w0, w1, w2, out):
         w2_raw = stage_2[:, 0, :].rearrange("p (j c) -> p j c", c=C)
         w2_grouped = stage_2[:, 1, :]
 
-        load_x(0, 0, CHUNK, 4)
+        load_x(0)
         nc.sync.dma_start(
             out=w1_raw.rearrange("p (v e) n -> p v e n", e=PAIR),
             in_=w1.rearrange("(v p e) n -> p v e n", p=P, e=PAIR),
         )
-        load_x(0, CHUNK, CHUNK, 1)
+        load_x(1)
         nc.sync.dma_start(out=w2_raw, in_=w2.rearrange("(j p) c -> p j c", p=P))
-        load_x(1, 0, T, 2)
+        load_x(2)
+        load_x(3)
+        load_x(4)
 
         ident_f32 = keep.tile([P, P], F32, name="ident_f32")
         make_identity(nc, ident_f32[:])
@@ -146,7 +152,7 @@ def tile_full_tmix_params_pc_t_kernel(tc, x, x_w, w0, w1, w2, out):
             for t in range(n // P):
                 nc.tensor.transpose(
                     out=banks[u][:, P * t : P * (t + 1)],
-                    in_=x_tiles[b][:, t0 // P + t, P * cb : P * (cb + PAIR)].bitcast(F32),
+                    in_=x_tiles[b * CHUNKS + t0 // CHUNK, cb // PAIR][:, t, :].bitcast(F32),
                     identity=ident_f32[:],
                 )
 
@@ -231,7 +237,6 @@ def tile_full_tmix_params_pc_t_kernel(tc, x, x_w, w0, w1, w2, out):
                 item[1](*item[2:])
 
         step = [0]
-        last_units = [(CHUNK, CHUNK, C_BLOCKS - 2, 2)]
 
         def advance():
             u = step[0]
@@ -239,10 +244,9 @@ def tile_full_tmix_params_pc_t_kernel(tc, x, x_w, w0, w1, w2, out):
             if u < len(units):
                 if u > HEAD_UNITS:
                     transpose_unit(u + T_AHEAD)
-                if u + T_AHEAD < len(units) and units[u + T_AHEAD][1:] in last_units:
-                    b = units[u + T_AHEAD][0] + 2
-                    if b < B:
-                        load_x(b, 0, T, 2)
+                k = (u + T_AHEAD) // HEAD_UNITS + 4
+                if (u + T_AHEAD) % HEAD_UNITS == HEAD_UNITS - 1 and k < B * CHUNKS:
+                    load_x(k)
                 scale_unit(u + C_AHEAD)
                 mix_unit(u)
             run_later(u)
@@ -326,7 +330,13 @@ def tile_full_tmix_params_pc_t_kernel(tc, x, x_w, w0, w1, w2, out):
                 out=results[0][:, BANK * half : BANK * (half + 1)], in_=acc[:], func=ACT.Ln,
                 scale=math.exp(-0.5),
             )
-            if half == 1:
+            if b == B - 1 and t == T // P - 1:
+                columns_of_half = slice(BANK * half, BANK * (half + 1))
+                nc.sync.dma_start(
+                    out=out[b, P * t : P * (t + 1), columns_of_half],
+                    in_=results[0][:, columns_of_half],
+                )
+            elif half == 1:
                 nc.sync.dma_start(out=out[b, P * t : P * (t + 1), :], in_=results[0][:])
 
         w1_rows = w1_raw.rearrange("p (g j) n -> p g n j", j=PACK)

@@ -321,11 +321,15 @@ def tile_full_tmix_params_pc_t_kernel(tc, x, x_w, w0, w1, w2, out):
                 results[0] = res_pool.tile([P, C], F32, name="result", tag="result")
             acc = psum_acc.tile([P, BANK], F32, name="o_acc", tag="acc")
             for k in range(BANK // P):
-                nc.tensor.transpose(
-                    out=acc[:, P * k : P * (k + 1)],
-                    in_=gate[b, c][:, (BANK // P) * half + k, P * i : P * (i + 1)],
-                    identity=ident_f32[:],
-                )
+                block = gate[b, c][:, (BANK // P) * half + k, P * i : P * (i + 1)]
+                if k == 0:
+                    nc.tensor.matmul(
+                        out=acc[:, 0:P], lhsT=block, rhs=ident_f32[:], start=True, stop=True
+                    )
+                else:
+                    nc.tensor.transpose(
+                        out=acc[:, P * k : P * (k + 1)], in_=block, identity=ident_f32[:]
+                    )
             nc.scalar.activation(
                 out=results[0][:, BANK * half : BANK * (half + 1)], in_=acc[:], func=ACT.Ln,
                 scale=math.exp(-0.5),

@@ -15,30 +15,23 @@ P = 128
 PACK = 4
 B, T, C, DW = 4, 1024, 1024, 512
 C_BLOCKS = C // P
-K1_PASSES = C // (P * PACK)
+PASSES = C // (P * PACK)
+PAIR = 2
+UNITS = C // (PAIR * P)
+BANK = 512
 CHUNK = 512
 CHUNKS = T // CHUNK
 TILES = CHUNK // P
-BANK = 512
 PAD = 8
-HEAD_NAMES = ("x_0", "x_1", "x_2", "x_3")
-PAIR = 2
-PIECE = 512
-HEAD_UNITS = C_BLOCKS // 2
-FEED_PLACES = (("h", 0), ("h", 2), ("z", 1), ("z", 4))
+
 ROUNDS = ((0, 1), (2, 3, 4), (5, 6, 7))
-G_LAG = 0
-G_HALVES = (0, 1)
-Q_LAG = (2, 1)
-START = (("h", 0, 0), ("q", 0, 0), ("z", 0, 0), ("z", 0, 1), ("h", 1, 2), ("q", 1, 0), ("z", 1, 2), ("z", 1, 5))
-V_FROM = 8
-SPACING = 5.3
-LOAD = 4
+X_BUFS = 4
+AHEAD = 3
+BANKS_A_UNIT = 5.3
+TABLE_BANKS = 4
+FIRST_ROUND = ((0, 4, 5, 6), (2, 4, 7, 10))
 HELD = 3
-LIMIT = (34, 34, 34, 34)
-ROUND = 2
-T_AHEAD = 3
-C_AHEAD = 1
+SCALAR_UNIT = 5 * UNITS
 
 FLOPS = 2 * B * T * (C * DW + DW * C)
 
@@ -46,9 +39,9 @@ FLOPS = 2 * B * T * (C * DW + DW * C)
 def tile_full_tmix_params_pc_t_kernel(tc, x, x_w, w0, w1, w2, out):
     nc = tc.nc
     with tc.manual_schedule(), tc.tile_pool(name="keep", bufs=1) as keep, tc.tile_pool(
-        name="xin", bufs=4
+        name="xin", bufs=X_BUFS
     ) as xin_pool, tc.tile_pool(name="codes", bufs=2) as codes_pool, tc.tile_pool(
-        name="gates", bufs=3
+        name="gates", bufs=max(len(chunks) for chunks in ROUNDS)
     ) as gate_pool, tc.tile_pool(
         name="res", bufs=7
     ) as res_pool, tc.psum_pool(name="psx", bufs=4) as psum_x, tc.psum_pool(
@@ -58,36 +51,40 @@ def tile_full_tmix_params_pc_t_kernel(tc, x, x_w, w0, w1, w2, out):
         nc.vector.memset(table_warm[:], 0.0)
         nc.scalar.activation(out=table_warm[:], in_=table_warm[:], func=ACT.Sigmoid)
 
-        vectors = keep.tile([P, 3, P], BF16, name="vectors")
+        vectors = keep.tile([P, PAIR + 1, P], BF16, name="vectors")
         nc.vector.memset(vectors[:], 0.0)
-        x_w_rows = vectors[:, 0:2, :].rearrange("p a c -> p (a c)")
-        w0_rows = vectors[:, 2, :]
+        x_w_rows = vectors[:, 0:PAIR, :].rearrange("p a c -> p (a c)")
+        w0_rows = vectors[:, PAIR, :]
         nc.sync.dma_start(
-            out=x_w_rows[0 : C_BLOCKS // PAIR, :], in_=x_w.rearrange("(r c) -> r c", c=PAIR * P)
+            out=x_w_rows[0:UNITS, :], in_=x_w.rearrange("(r c) -> r c", c=PAIR * P)
         )
         nc.sync.dma_start(out=w0_rows[0:C_BLOCKS, :], in_=w0.rearrange("(r c) -> r c", c=P))
-        x_tiles = {}
+
+        x_units = {}
 
         def load_x(k):
             b, c = divmod(k, CHUNKS)
             rows = x[b, CHUNK * c : CHUNK * (c + 1), :].rearrange("(t p) c -> p t c", p=P)
-            width = PAIR * P if k == 0 else C
-            for c0 in range(0, C, width):
-                pool = keep if k == 0 else xin_pool
-                name = HEAD_NAMES[c0 // width] if k == 0 else "x_sb"
-                tile = pool.tile([P, TILES, width], BF16, name=name, tag=name)
-                nc.sync.dma_start(out=tile[:], in_=rows[:, :, c0 : c0 + width])
-                for v in range(width // (PAIR * P)):
-                    x_tiles[k, (c0 + v * PAIR * P) // (PAIR * P)] = tile[
-                        :, :, PAIR * P * v : PAIR * P * (v + 1)
-                    ]
+            if k == 0:
+                for v in range(UNITS):
+                    name = ("x_0", "x_1", "x_2", "x_3")[v]
+                    tile = keep.tile([P, TILES, PAIR * P], BF16, name=name)
+                    nc.sync.dma_start(
+                        out=tile[:], in_=rows[:, :, PAIR * P * v : PAIR * P * (v + 1)]
+                    )
+                    x_units[v] = tile[:]
+            else:
+                tile = xin_pool.tile([P, TILES, C], BF16, name="x_sb", tag="x_sb")
+                nc.sync.dma_start(out=tile[:], in_=rows)
+                for v in range(UNITS):
+                    x_units[UNITS * k + v] = tile[:, :, PAIR * P * v : PAIR * P * (v + 1)]
 
         stage_1 = gate_pool.tile([P, 2, PACK * C], BF16, name="stage_1", tag="gate", align_bytes=64)
         stage_2 = gate_pool.tile([P, 2, PACK * C], BF16, name="stage_2", tag="gate", align_bytes=64)
         w1_raw = stage_1[:, 0, :].rearrange("p (r n) -> p r n", n=DW)
-        w1_grouped = stage_1[:, 1, :].rearrange("p (g n) -> p g n", g=K1_PASSES)
-        w2_raw = stage_2[:, 0, :].rearrange("p (j c) -> p j c", c=C)
-        w2_grouped = stage_2[:, 1, :]
+        w1_grouped = stage_1[:, 1, :].rearrange("p (g n j) -> p g n j", g=PASSES, j=PACK)
+        w2_raw = stage_2[:, 0, :].rearrange("p (j c) -> p c j", c=C)
+        w2_grouped = stage_2[:, 1, :].rearrange("p (c j) -> p c j", j=PACK)
 
         load_x(0)
         nc.sync.dma_start(
@@ -95,10 +92,12 @@ def tile_full_tmix_params_pc_t_kernel(tc, x, x_w, w0, w1, w2, out):
             in_=w1.rearrange("(v p e) n -> p v e n", p=P, e=PAIR),
         )
         load_x(1)
-        nc.sync.dma_start(out=w2_raw, in_=w2.rearrange("(j p) c -> p j c", p=P))
-        load_x(2)
-        load_x(3)
-        load_x(4)
+        nc.sync.dma_start(
+            out=stage_2[:, 0, :].rearrange("p (j c) -> p j c", c=C),
+            in_=w2.rearrange("(j p) c -> p j c", p=P),
+        )
+        for k in range(2, X_BUFS + 1):
+            load_x(k)
 
         ident_f32 = keep.tile([P, P], F32, name="ident_f32")
         make_identity(nc, ident_f32[:])
@@ -108,9 +107,7 @@ def tile_full_tmix_params_pc_t_kernel(tc, x, x_w, w0, w1, w2, out):
         columns = keep.tile([P, 2 * C_BLOCKS], F32, name="columns")
         x_w_t = psum_acc.tile([P, P], F32, name="x_w_t", tag="acc")
         nc.tensor.transpose(out=x_w_t[:], in_=x_w_rows.bitcast(F32), identity=ident_f32[:])
-        nc.vector.tensor_copy(
-            out=columns[:, 0:C_BLOCKS], in_=x_w_t[:, 0 : C_BLOCKS // PAIR].bitcast(BF16)
-        )
+        nc.vector.tensor_copy(out=columns[:, 0:C_BLOCKS], in_=x_w_t[:, 0:UNITS].bitcast(BF16))
         w0_t = psum_acc.tile([P, P], BF16, name="w0_t", tag="acc")
         nc.tensor.transpose(out=w0_t[:], in_=w0_rows, identity=ident_bf[:])
         nc.vector.tensor_copy(out=columns[:, C_BLOCKS : 2 * C_BLOCKS], in_=w0_t[:, 0:C_BLOCKS])
@@ -121,150 +118,144 @@ def tile_full_tmix_params_pc_t_kernel(tc, x, x_w, w0, w1, w2, out):
             out=keep_share[:], in0=mix, scalar1=-1.0, scalar2=1.0, op0=ALU.mult, op1=ALU.add
         )
 
-        w1_codes = keep.tile([P, K1_PASSES, DW], U32, name="w1_codes", align_bytes=64)
-        w1_scales = keep.tile([P, K1_PASSES, DW], U8, name="w1_scales", align_bytes=64)
+        w1_codes = keep.tile([P, PASSES, DW], U32, name="w1_codes", align_bytes=64)
+        w1_scales = keep.tile([P, PASSES, DW], U8, name="w1_scales", align_bytes=64)
         w2_codes = keep.tile([P, C], U32, name="w2_codes", align_bytes=64)
         w2_scales = keep.tile([P, C], U8, name="w2_scales", align_bytes=64)
 
-        carried = keep.tile([P, C_BLOCKS // PAIR, PAIR * (PAD + T)], F32, name="carried")
+        carried = keep.tile([P, UNITS, PAIR * (PAD + T)], F32, name="carried")
         by_channel = carried[:].rearrange("p v (e t) -> p (v e) t", e=PAIR)
         by_token = carried[:].rearrange("p v (t e) -> p v t e", e=PAIR)
         nc.vector.memset(by_channel[:, :, 0:PAD], 0.0)
         planes = keep.tile([P, C_BLOCKS, T], BF16, name="planes")
-        grouped = keep.tile([P, K1_PASSES, T, PACK], BF16, name="grouped", align_bytes=64)
-
-        units = []
-        for b in range(B):
-            for t0 in range(0, T, CHUNK):
-                for cb in range(0, C_BLOCKS, 2):
-                    units.append((b, t0, CHUNK, cb, 2))
-        scalar_lates = [u for u in range(4 * HEAD_UNITS) if u < HEAD_UNITS or u < 8]
+        grouped = keep.tile([P, PASSES, T, PACK], BF16, name="grouped", align_bytes=64)
         banks = {}
         xw_codes = {}
         xw_scales = {}
-        later = []
+        last_unit = UNITS * B * CHUNKS
 
         def transpose_unit(u):
-            if u >= len(units):
-                return
-            b, t0, n, cb, k = units[u]
-            banks[u] = psum_x.tile([P, n], F32, name="xt", tag="xt")
-            for t in range(n // P):
-                nc.tensor.transpose(
-                    out=banks[u][:, P * t : P * (t + 1)],
-                    in_=x_tiles[b * CHUNKS + t0 // CHUNK, cb // PAIR][:, t, :].bitcast(F32),
-                    identity=ident_f32[:],
-                )
+            if u < last_unit:
+                banks[u] = psum_x.tile([P, CHUNK], F32, name="xt", tag="xt")
+                for i in range(TILES):
+                    nc.tensor.transpose(
+                        out=banks[u][:, P * i : P * (i + 1)],
+                        in_=x_units[u][:, i, :].bitcast(F32),
+                        identity=ident_f32[:],
+                    )
 
         def pairs(u):
             return banks[u][:].bitcast(BF16).rearrange("p (t e) -> p t e", e=PAIR)
 
         def scale_unit(u):
-            if u >= len(units):
+            if u >= last_unit:
                 return
-            b, t0, n, cb, k = units[u]
-            if u in scalar_lates:
-                for e in range(PAIR):
+            k, v = divmod(u, UNITS)
+            b, c = divmod(k, CHUNKS)
+            tokens = slice(PAD + CHUNK * c, PAD + CHUNK * (c + 1))
+            if b == 0 or u == SCALAR_UNIT:
+                if b > 0:
+                    before = PAD - 1 + CHUNK * c
+                    nc.vector.tensor_copy(
+                        out=by_channel[:, PAIR * v : PAIR * (v + 1), before],
+                        in_=by_token[:, v, before, :],
+                    )
+                for cb in range(PAIR * v, PAIR * (v + 1)):
                     nc.scalar.activation(
-                        out=by_channel[:, cb + e, PAD + t0 : PAD + t0 + n],
-                        in_=pairs(u)[:, :, e], func=ACT.Copy, scale=mix[:, cb + e : cb + e + 1],
+                        out=by_channel[:, cb, tokens], in_=pairs(u)[:, :, cb % PAIR],
+                        func=ACT.Copy, scale=mix[:, cb : cb + 1],
                     )
                 return
-            if b == 1 and t0 == 0:
-                nc.vector.memset(by_token[:, cb // PAIR, PAD - 1 : PAD, :], 0.0)
+            if b == 1 and c == 0:
+                nc.vector.memset(by_token[:, v, PAD - 1 : PAD, :], 0.0)
+            weights = mix[:, PAIR * v : PAIR * (v + 1)].unsqueeze(1)
             nc.vector.tensor_tensor(
-                out=by_token[:, cb // PAIR, PAD + t0 : PAD + t0 + n, :], in0=pairs(u),
-                in1=mix[:, cb : cb + PAIR].unsqueeze(1).to_broadcast([P, n, PAIR]), op=ALU.mult,
+                out=by_token[:, v, tokens, :], in0=pairs(u),
+                in1=weights.to_broadcast([P, CHUNK, PAIR]), op=ALU.mult,
             )
 
         def mix_unit(u):
-            b, t0, n, cb, k = units[u]
+            k, v = divmod(u, UNITS)
+            b, c = divmod(k, CHUNKS)
+            earlier = slice(PAD - 1 + CHUNK * c, PAD - 1 + CHUNK * (c + 1))
             for e in range(PAIR):
-                earlier = slice(PAD - 1 + t0, PAD - 1 + t0 + n)
+                cb = PAIR * v + e
                 nc.vector.scalar_tensor_tensor(
-                    out=planes[:, cb + e, t0 : t0 + n], in0=pairs(u)[:, :, e],
-                    scalar=keep_share[:, cb + e : cb + e + 1],
-                    in1=by_channel[:, cb + e, earlier] if b == 0
-                    else by_token[:, cb // PAIR, earlier, e],
+                    out=planes[:, cb, CHUNK * c : CHUNK * (c + 1)], in0=pairs(u)[:, :, e],
+                    scalar=keep_share[:, cb : cb + 1],
+                    in1=by_channel[:, cb, earlier] if b == 0 or u == SCALAR_UNIT
+                    else by_token[:, v, earlier, e],
                     op0=ALU.mult, op1=ALU.add,
                 )
-            if (cb + k) % PACK == 0:
-                g = cb // PACK
-                for p0 in range(t0, t0 + n, PIECE):
-                    later.append((u + G_LAG if u >= HEAD_UNITS else HEAD_UNITS - 1, regroup, b, g, slice(p0, p0 + PIECE), u >= HEAD_UNITS and (g == 0 or 2 * HEAD_UNITS <= u < V_FROM and g in G_HALVES)))
-                    later.append((u + (Q_LAG[g] if 2 * HEAD_UNITS <= u < V_FROM else (2, 0)[g]) if u >= HEAD_UNITS else HEAD_UNITS - 1, quantise_x, b, g, slice(p0, p0 + PIECE), False))
-            if cb == 0 and t0 == 0:
+            if v == UNITS // 2 - 1 and k > 0:
+                regroup_by_gpsimd(c, 0)
+            if v == UNITS - 1:
+                for g in range(0 if k == 0 else 1, PASSES):
+                    regroup_by_vector(c, g)
+                for g in range(PASSES):
+                    quantise_x(b, c, g)
+
+        def planes_of(c, g):
+            return planes[:, PACK * g : PACK * (g + 1), CHUNK * c : CHUNK * (c + 1)]
+
+        def regroup_by_gpsimd(c, g):
+            nc.gpsimd.tensor_scalar(
+                out=grouped[:, g, CHUNK * c : CHUNK * (c + 1), :],
+                in0=planes_of(c, g).rearrange("p j t -> p t j"),
+                scalar1=1.0, scalar2=0.0, op0=ALU.mult, op1=ALU.add,
+            )
+
+        def regroup_by_vector(c, g):
+            nc.vector.tensor_copy(
+                out=grouped[:, g, CHUNK * c : CHUNK * (c + 1), :].rearrange(
+                    "p (t i) j -> p t j i", i=4
+                ),
+                in_=planes_of(c, g).rearrange("p j (t i) -> p t j i", i=4),
+            )
+
+        def quantise_x(b, c, g):
+            if b not in xw_codes:
                 xw_codes[b] = codes_pool.tile(
-                    [P, K1_PASSES, T], U32, name="xw_codes", tag="xw_codes", align_bytes=64
+                    [P, PASSES, T], U32, name="xw_codes", tag="xw_codes", align_bytes=64
                 )
                 xw_scales[b] = codes_pool.tile(
-                    [P, K1_PASSES, T], U8, name="xw_scales", tag="xw_scales", align_bytes=64
+                    [P, PASSES, T], U8, name="xw_scales", tag="xw_scales", align_bytes=64
                 )
-
-        def regroup(b, g, tokens, on_gpsimd):
-            if on_gpsimd:
-                nc.gpsimd.tensor_scalar(
-                    out=grouped[:, g, tokens, :],
-                    in0=planes[:, PACK * g : PACK * (g + 1), tokens].rearrange("p j t -> p t j"),
-                    scalar1=1.0, scalar2=0.0, op0=ALU.mult, op1=ALU.add,
-                )
-            else:
-                nc.vector.tensor_copy(
-                    out=grouped[:, g, tokens, :].rearrange("p (c i) j -> p c j i", i=4),
-                    in_=planes[:, PACK * g : PACK * (g + 1), tokens].rearrange(
-                        "p j (c i) -> p c j i", i=4
-                    ),
-                )
-
-        def quantise_x(b, g, tokens, unused):
+            tokens = slice(CHUNK * c, CHUNK * (c + 1))
             nc.vector.quantize_mx(
                 out=xw_codes[b][:, g, tokens].bitcast(FP8X4),
                 scales=xw_scales[b][:, g, tokens],
-                in_=grouped[:, g, tokens, :].rearrange("p c j -> p (c j)"),
+                in_=grouped[:, g, tokens, :].rearrange("p t j -> p (t j)"),
             )
 
-        def run_later(u):
-            due = [item for item in later if item[0] <= u]
-            for item in [i for i in due if i[1] is regroup] + [i for i in due if i[1] is not regroup]:
-                later.remove(item)
-                item[1](*item[2:])
-
-        def finish_chunk(b, c):
-            chunk = slice(CHUNK * c, CHUNK * (c + 1))
-            due = [item for item in later if item[2] == b and item[4] == chunk]
-            for item in [i for i in due if i[1] is regroup] + [i for i in due if i[1] is not regroup]:
-                later.remove(item)
-                item[1](*item[2:])
-
-        step = [0]
+        mixed = [0]
 
         def advance():
-            u = step[0]
-            step[0] = u + 1
-            if u < len(units):
-                if u > HEAD_UNITS:
-                    transpose_unit(u + T_AHEAD)
-                k = (u + T_AHEAD) // HEAD_UNITS + 4
-                if (u + T_AHEAD) % HEAD_UNITS == HEAD_UNITS - 1 and k < B * CHUNKS:
-                    load_x(k)
-                scale_unit(u + C_AHEAD)
-                mix_unit(u)
-            run_later(u)
+            u = mixed[0]
+            mixed[0] = u + 1
+            k, v = divmod(u, UNITS)
+            if u > UNITS:
+                transpose_unit(u + AHEAD)
+            if v == 0 and k + X_BUFS < B * CHUNKS:
+                load_x(k + X_BUFS)
+            scale_unit(u + 1)
+            mix_unit(u)
 
         h_grouped = {}
         h_codes = {}
         h_scales = {}
         gate = {}
 
-        def hidden(b, c, i):
+        def hidden(k, i):
+            b, c = divmod(k, CHUNKS)
             if i == 0:
-                h_grouped[c] = codes_pool.tile(
+                h_grouped[k] = codes_pool.tile(
                     [P, CHUNK, PACK], BF16, name="h_grouped", tag="h_grouped", align_bytes=64
                 )
             acc = psum_acc.tile([P, PACK, P], F32, name="h_acc", tag="acc")
             tokens = slice(CHUNK * c + P * i, CHUNK * c + P * (i + 1))
             for m in range(PACK):
-                for g in range(K1_PASSES):
+                for g in range(PASSES):
                     nc.tensor.matmul_mx(
                         out=acc[:, m, :],
                         lhsT=w1_codes[:, g, P * m : P * (m + 1)].bitcast(FP8X4),
@@ -272,30 +263,30 @@ def tile_full_tmix_params_pc_t_kernel(tc, x, x_w, w0, w1, w2, out):
                         rhs=xw_codes[b][:, g, tokens].bitcast(FP8X4),
                         rhs_scale=xw_scales[b][:, g, tokens],
                         start=(g == 0),
-                        stop=(g == K1_PASSES - 1),
+                        stop=(g == PASSES - 1),
                     )
             nc.scalar.activation(
-                out=h_grouped[c][:, P * i : P * (i + 1), :],
+                out=h_grouped[k][:, P * i : P * (i + 1), :],
                 in_=acc[:].rearrange("p m t -> p t m"),
                 func=ACT.Tanh,
             )
 
-        def quantise_hidden(c):
-            h_codes[c] = codes_pool.tile(
+        def quantise_hidden(k):
+            h_codes[k] = codes_pool.tile(
                 [P, CHUNK], U32, name="h_codes", tag="h_codes", align_bytes=64
             )
-            h_scales[c] = codes_pool.tile(
+            h_scales[k] = codes_pool.tile(
                 [P, CHUNK], U8, name="h_scales", tag="h_scales", align_bytes=64
             )
             nc.vector.quantize_mx(
-                out=h_codes[c][:].bitcast(FP8X4),
-                scales=h_scales[c][:],
-                in_=h_grouped[c][:].rearrange("p t j -> p (t j)"),
+                out=h_codes[k][:].bitcast(FP8X4),
+                scales=h_scales[k][:],
+                in_=h_grouped[k][:].rearrange("p t j -> p (t j)"),
             )
 
-        def gates(b, c, cs):
+        def gates(k, cs):
             if cs == 0:
-                gate[b, c] = gate_pool.tile(
+                gate[k] = gate_pool.tile(
                     [P, C_BLOCKS, CHUNK], F32, name="gate", tag="gate", align_bytes=64
                 )
             acc = psum_acc.tile([P, CHUNK], F32, name="z_acc", tag="acc")
@@ -303,134 +294,117 @@ def tile_full_tmix_params_pc_t_kernel(tc, x, x_w, w0, w1, w2, out):
                 out=acc[:],
                 lhsT=w2_codes[:, P * cs : P * (cs + 1)].bitcast(FP8X4),
                 lhsT_scale=w2_scales[:, P * cs : P * (cs + 1)],
-                rhs=h_codes[c][:].bitcast(FP8X4),
-                rhs_scale=h_scales[c][:],
+                rhs=h_codes[k][:].bitcast(FP8X4),
+                rhs_scale=h_scales[k][:],
                 start=True,
                 stop=True,
             )
             nc.scalar.activation(
-                out=gate[b, c][:, cs, :], in_=acc[:], func=ACT.Sigmoid,
-                bias=bias[:, cs : cs + 1], scale=1.0,
+                out=gate[k][:, cs, :], in_=acc[:], func=ACT.Sigmoid, bias=bias[:, cs : cs + 1],
+                scale=1.0,
             )
 
         results = {}
 
-        def output(b, c, i, half):
-            t = TILES * c + i
+        def output(k, i, half):
+            b, c = divmod(k, CHUNKS)
             if half == 0:
-                results[0] = res_pool.tile([P, C], F32, name="result", tag="result")
+                results[i] = res_pool.tile([P, C], F32, name="result", tag="result")
             acc = psum_acc.tile([P, BANK], F32, name="o_acc", tag="acc")
-            for k in range(BANK // P):
-                block = gate[b, c][:, (BANK // P) * half + k, P * i : P * (i + 1)]
-                if k == 0:
+            for j in range(BANK // P):
+                block = gate[k][:, (BANK // P) * half + j, P * i : P * (i + 1)]
+                if j == 0:
                     nc.tensor.matmul(
                         out=acc[:, 0:P], lhsT=block, rhs=ident_f32[:], start=True, stop=True
                     )
                 else:
                     nc.tensor.transpose(
-                        out=acc[:, P * k : P * (k + 1)], in_=block, identity=ident_f32[:]
+                        out=acc[:, P * j : P * (j + 1)], in_=block, identity=ident_f32[:]
                     )
+            channels = slice(BANK * half, BANK * (half + 1))
             nc.scalar.activation(
-                out=results[0][:, BANK * half : BANK * (half + 1)], in_=acc[:], func=ACT.Ln,
-                scale=math.exp(-0.5),
+                out=results[i][:, channels], in_=acc[:], func=ACT.Ln, scale=math.exp(-0.5)
             )
-            if b == B - 1 and t == T // P - 1:
-                columns_of_half = slice(BANK * half, BANK * (half + 1))
-                nc.sync.dma_start(
-                    out=out[b, P * t : P * (t + 1), columns_of_half],
-                    in_=results[0][:, columns_of_half],
-                )
+            rows = slice(CHUNK * c + P * i, CHUNK * c + P * (i + 1))
+            if k == B * CHUNKS - 1 and i == TILES - 1:
+                nc.sync.dma_start(out=out[b, rows, channels], in_=results[i][:, channels])
             elif half == 1:
-                nc.sync.dma_start(out=out[b, P * t : P * (t + 1), :], in_=results[0][:])
+                nc.sync.dma_start(out=out[b, rows, :], in_=results[i][:])
 
-        w1_rows = w1_raw.rearrange("p (g j) n -> p g n j", j=PACK)
-        w1_cols = w1_grouped.rearrange("p g (n j) -> p g n j", j=PACK)
-        for u in range(HEAD_UNITS):
+        for u in range(UNITS):
             transpose_unit(u)
-        for u in range(HEAD_UNITS):
+        for u in range(UNITS):
             scale_unit(u)
+        w1_planes = w1_raw.rearrange("p (g j) n -> p g n j", j=PACK)
         nc.gpsimd.tensor_scalar(
-            out=w1_cols[:, 1], in0=w1_rows[:, 1], scalar1=1.0, scalar2=0.0, op0=ALU.mult, op1=ALU.add
+            out=w1_grouped[:, 1], in0=w1_planes[:, 1], scalar1=1.0, scalar2=0.0, op0=ALU.mult,
+            op1=ALU.add,
         )
-        nc.scalar.copy(out=w1_cols[:, 0], in_=w1_rows[:, 0])
-        for u in range(HEAD_UNITS):
+        nc.scalar.copy(out=w1_grouped[:, 0], in_=w1_planes[:, 0])
+        for u in range(UNITS):
             mix_unit(u)
-            run_later(u)
-            transpose_unit(u + HEAD_UNITS)
-        step[0] = HEAD_UNITS
-        for g in range(K1_PASSES):
+            transpose_unit(UNITS + u)
+        mixed[0] = UNITS
+        for g in range(PASSES):
             nc.vector.quantize_mx(
                 out=w1_codes[:, g, :].bitcast(FP8X4),
                 scales=w1_scales[:, g, :],
-                in_=w1_grouped[:, g, :],
+                in_=w1_grouped[:, g].rearrange("p n j -> p (n j)"),
             )
-        w2_rows = w2_raw.rearrange("p j c -> p c j")
-        w2_cols = w2_grouped.rearrange("p (c j) -> p c j", j=PACK)
-        nc.scalar.copy(out=w2_cols[:, 0 : C // 2], in_=w2_rows[:, 0 : C // 2])
+        nc.scalar.copy(out=w2_grouped[:, 0 : C // 2], in_=w2_raw[:, 0 : C // 2])
         nc.vector.tensor_copy(
-            out=w2_cols[:, C // 2 :].rearrange("p (c i) j -> p c j i", i=4),
-            in_=w2_raw[:, :, C // 2 :].rearrange("p j (c i) -> p c j i", i=4),
+            out=w2_grouped[:, C // 2 : C].rearrange("p (c i) j -> p c j i", i=4),
+            in_=w2_raw[:, C // 2 : C].rearrange("p (c i) j -> p c j i", i=4),
         )
-        for u in range(C_AHEAD):
-            scale_unit(HEAD_UNITS + u)
-
-        def quantise_w2():
-            nc.vector.quantize_mx(
-                out=w2_codes[:].bitcast(FP8X4), scales=w2_scales[:], in_=w2_grouped
-            )
-
-        slots = [0]
+        scale_unit(UNITS)
 
         credit = [0.0]
 
-        def feed(slots_passed):
-            credit[0] += slots_passed
-            while credit[0] >= SPACING and step[0] < len(units) + 2:
-                credit[0] -= SPACING
+        def feed(scalar_banks):
+            credit[0] += scalar_banks
+            while credit[0] >= BANKS_A_UNIT and mixed[0] < last_unit:
+                credit[0] -= BANKS_A_UNIT
                 advance()
 
-        def stage_order(r):
-            chunks = [divmod(k, CHUNKS) for k in ROUNDS[r]]
-            tanh = [[("h", bc, i) for i in range(TILES)] + [("q", bc, 0)] for bc in chunks]
-            sigmoid = [[("z", bc, cs) for cs in range(C_BLOCKS)] for bc in chunks]
-            if r == 0:
+        def steps(chunks):
+            tanh = [[("h", k, i) for i in range(TILES)] + [("q", k, 0)] for k in chunks]
+            sigmoid = [[("z", k, cs) for cs in range(C_BLOCKS)] for k in chunks]
+            if len(chunks) == 2:
                 return tanh[0] + sigmoid[0] + tanh[1] + sigmoid[1]
-            order = tanh[0] + tanh[1]
-            for k in range(len(chunks)):
-                if k == 0:
-                    order += sigmoid[0]
-                elif k + 1 < len(chunks):
-                    order += sigmoid[k][: C_BLOCKS - HELD] + tanh[k + 1] + sigmoid[k][C_BLOCKS - HELD :]
-                else:
-                    order += sigmoid[k]
-            return order
+            free = C_BLOCKS - HELD
+            return (
+                tanh[0] + tanh[1] + sigmoid[0]
+                + sigmoid[1][:free] + tanh[2] + sigmoid[1][free:] + sigmoid[2]
+            )
 
-        for r, bs in enumerate(ROUNDS):
+        for r, chunks in enumerate(ROUNDS):
             if r > 0:
-                feed(LOAD)
+                feed(TABLE_BANKS)
                 nc.scalar.activation(out=table_warm[:], in_=columns[:, 0:1], func=ACT.Sigmoid)
-            for kind, (b, c), i in stage_order(r):
-                if b == 0:
-                    if (kind, c, i) in START:
+            for n, (kind, k, i) in enumerate(steps(chunks)):
+                if r == 0:
+                    chunk, position = divmod(n, TILES + 1 + C_BLOCKS)
+                    if position in FIRST_ROUND[chunk]:
                         advance()
                 elif kind != "q":
                     feed(1)
                 if kind == "h":
-                    if i == 0:
-                        while not any(x[0] == b and x[1] + x[2] >= CHUNK * (c + 1) and x[3] + x[4] == C_BLOCKS for x in units[: step[0]]):
-                            advance()
-                        finish_chunk(b, c)
-                    hidden(b, c, i)
+                    while mixed[0] < UNITS * (k + 1):
+                        advance()
+                    hidden(k, i)
                 elif kind == "q":
-                    if r == 0 and c == 0:
-                        quantise_w2()
-                    quantise_hidden(c)
+                    if k == 0:
+                        nc.vector.quantize_mx(
+                            out=w2_codes[:].bitcast(FP8X4),
+                            scales=w2_scales[:],
+                            in_=w2_grouped.rearrange("p c j -> p (c j)"),
+                        )
+                    quantise_hidden(k)
                 else:
-                    gates(b, c, i)
-            feed(LOAD)
-            for k in bs:
-                b, c = divmod(k, CHUNKS)
+                    gates(k, i)
+            feed(TABLE_BANKS)
+            for k in chunks:
                 for i in range(TILES):
-                    for half in range(2):
+                    for half in range(C // BANK):
                         feed(1)
-                        output(b, c, i, half)
+                        output(k, i, half)

import math

from concourse import mybir
from concourse.masks import make_identity

F32 = mybir.dt.float32
BF16 = mybir.dt.bfloat16
U32 = mybir.dt.uint32
U8 = mybir.dt.uint8
FP8X4 = mybir.dt.float8_e4m3fn_x4
ACT = mybir.ActivationFunctionType
ALU = mybir.AluOpType

P = 128
PACK = 4
B, T, C, DW = 4, 1024, 1024, 512
C_BLOCKS = C // P
PASSES = C // (P * PACK)
PAIR = 2
UNITS = C // (PAIR * P)
BANK = 512
CHUNK = 512
CHUNKS = T // CHUNK
TILES = CHUNK // P
PAD = 8

ROUNDS = ((0, 1), (2, 3, 4), (5, 6, 7))
X_BUFS = 4
AHEAD = 3
BANKS_A_UNIT = 5.3
TABLE_BANKS = 4
FIRST_ROUND = ((0, 4, 5, 6), (2, 4, 7, 10))
HELD = 3
SCALAR_UNIT = 5 * UNITS

FLOPS = 2 * B * T * (C * DW + DW * C)


def tile_full_tmix_params_pc_t_kernel(tc, x, x_w, w0, w1, w2, out):
    nc = tc.nc
    with tc.manual_schedule(), tc.tile_pool(name="keep", bufs=1) as keep, tc.tile_pool(
        name="xin", bufs=X_BUFS
    ) as xin_pool, tc.tile_pool(name="codes", bufs=2) as codes_pool, tc.tile_pool(
        name="gates", bufs=max(len(chunks) for chunks in ROUNDS)
    ) as gate_pool, tc.tile_pool(
        name="res", bufs=7
    ) as res_pool, tc.psum_pool(name="psx", bufs=4) as psum_x, tc.psum_pool(
        name="psa", bufs=4
    ) as psum_acc:
        table_warm = keep.tile([P, 1], F32, name="table_warm")
        nc.vector.memset(table_warm[:], 0.0)
        nc.scalar.activation(out=table_warm[:], in_=table_warm[:], func=ACT.Sigmoid)

        vectors = keep.tile([P, PAIR + 1, P], BF16, name="vectors")
        nc.vector.memset(vectors[:], 0.0)
        x_w_rows = vectors[:, 0:PAIR, :].rearrange("p a c -> p (a c)")
        w0_rows = vectors[:, PAIR, :]
        nc.sync.dma_start(
            out=x_w_rows[0:UNITS, :], in_=x_w.rearrange("(r c) -> r c", c=PAIR * P)
        )
        nc.sync.dma_start(out=w0_rows[0:C_BLOCKS, :], in_=w0.rearrange("(r c) -> r c", c=P))

        x_units = {}

        def load_x(k):
            b, c = divmod(k, CHUNKS)
            rows = x[b, CHUNK * c : CHUNK * (c + 1), :].rearrange("(t p) c -> p t c", p=P)
            if k == 0:
                for v in range(UNITS):
                    name = ("x_0", "x_1", "x_2", "x_3")[v]
                    tile = keep.tile([P, TILES, PAIR * P], BF16, name=name)
                    nc.sync.dma_start(
                        out=tile[:], in_=rows[:, :, PAIR * P * v : PAIR * P * (v + 1)]
                    )
                    x_units[v] = tile[:]
            else:
                tile = xin_pool.tile([P, TILES, C], BF16, name="x_sb", tag="x_sb")
                nc.sync.dma_start(out=tile[:], in_=rows)
                for v in range(UNITS):
                    x_units[UNITS * k + v] = tile[:, :, PAIR * P * v : PAIR * P * (v + 1)]

        stage_1 = gate_pool.tile([P, 2, PACK * C], BF16, name="stage_1", tag="gate", align_bytes=64)
        stage_2 = gate_pool.tile([P, 2, PACK * C], BF16, name="stage_2", tag="gate", align_bytes=64)
        w1_raw = stage_1[:, 0, :].rearrange("p (r n) -> p r n", n=DW)
        w1_grouped = stage_1[:, 1, :].rearrange("p (g n j) -> p g n j", g=PASSES, j=PACK)
        w2_raw = stage_2[:, 0, :].rearrange("p (j c) -> p c j", c=C)
        w2_grouped = stage_2[:, 1, :].rearrange("p (c j) -> p c j", j=PACK)

        load_x(0)
        nc.sync.dma_start(
            out=w1_raw.rearrange("p (v e) n -> p v e n", e=PAIR),
            in_=w1.rearrange("(v p e) n -> p v e n", p=P, e=PAIR),
        )
        load_x(1)
        nc.sync.dma_start(
            out=stage_2[:, 0, :].rearrange("p (j c) -> p j c", c=C),
            in_=w2.rearrange("(j p) c -> p j c", p=P),
        )
        for k in range(2, X_BUFS + 1):
            load_x(k)

        ident_f32 = keep.tile([P, P], F32, name="ident_f32")
        make_identity(nc, ident_f32[:])
        ident_bf = keep.tile([P, P], BF16, name="ident_bf")
        make_identity(nc, ident_bf[:])

        columns = keep.tile([P, 2 * C_BLOCKS], F32, name="columns")
        x_w_t = psum_acc.tile([P, P], F32, name="x_w_t", tag="acc")
        nc.tensor.transpose(out=x_w_t[:], in_=x_w_rows.bitcast(F32), identity=ident_f32[:])
        nc.vector.tensor_copy(out=columns[:, 0:C_BLOCKS], in_=x_w_t[:, 0:UNITS].bitcast(BF16))
        w0_t = psum_acc.tile([P, P], BF16, name="w0_t", tag="acc")
        nc.tensor.transpose(out=w0_t[:], in_=w0_rows, identity=ident_bf[:])
        nc.vector.tensor_copy(out=columns[:, C_BLOCKS : 2 * C_BLOCKS], in_=w0_t[:, 0:C_BLOCKS])
        mix = columns[:, 0:C_BLOCKS]
        bias = columns[:, C_BLOCKS : 2 * C_BLOCKS]
        keep_share = keep.tile([P, C_BLOCKS], F32, name="keep_share")
        nc.vector.tensor_scalar(
            out=keep_share[:], in0=mix, scalar1=-1.0, scalar2=1.0, op0=ALU.mult, op1=ALU.add
        )

        w1_codes = keep.tile([P, PASSES, DW], U32, name="w1_codes", align_bytes=64)
        w1_scales = keep.tile([P, PASSES, DW], U8, name="w1_scales", align_bytes=64)
        w2_codes = keep.tile([P, C], U32, name="w2_codes", align_bytes=64)
        w2_scales = keep.tile([P, C], U8, name="w2_scales", align_bytes=64)

        carried = keep.tile([P, UNITS, PAIR * (PAD + T)], F32, name="carried")
        by_channel = carried[:].rearrange("p v (e t) -> p (v e) t", e=PAIR)
        by_token = carried[:].rearrange("p v (t e) -> p v t e", e=PAIR)
        nc.vector.memset(by_channel[:, :, 0:PAD], 0.0)
        planes = keep.tile([P, C_BLOCKS, T], BF16, name="planes")
        grouped = keep.tile([P, PASSES, T, PACK], BF16, name="grouped", align_bytes=64)
        banks = {}
        xw_codes = {}
        xw_scales = {}
        last_unit = UNITS * B * CHUNKS

        def transpose_unit(u):
            if u < last_unit:
                banks[u] = psum_x.tile([P, CHUNK], F32, name="xt", tag="xt")
                for i in range(TILES):
                    nc.tensor.transpose(
                        out=banks[u][:, P * i : P * (i + 1)],
                        in_=x_units[u][:, i, :].bitcast(F32),
                        identity=ident_f32[:],
                    )

        def pairs(u):
            return banks[u][:].bitcast(BF16).rearrange("p (t e) -> p t e", e=PAIR)

        def scale_unit(u):
            if u >= last_unit:
                return
            k, v = divmod(u, UNITS)
            b, c = divmod(k, CHUNKS)
            tokens = slice(PAD + CHUNK * c, PAD + CHUNK * (c + 1))
            if b == 0 or u == SCALAR_UNIT:
                if b > 0:
                    before = PAD - 1 + CHUNK * c
                    nc.vector.tensor_copy(
                        out=by_channel[:, PAIR * v : PAIR * (v + 1), before],
                        in_=by_token[:, v, before, :],
                    )
                for cb in range(PAIR * v, PAIR * (v + 1)):
                    nc.scalar.activation(
                        out=by_channel[:, cb, tokens], in_=pairs(u)[:, :, cb % PAIR],
                        func=ACT.Copy, scale=mix[:, cb : cb + 1],
                    )
                return
            if b == 1 and c == 0:
                nc.vector.memset(by_token[:, v, PAD - 1 : PAD, :], 0.0)
            weights = mix[:, PAIR * v : PAIR * (v + 1)].unsqueeze(1)
            nc.vector.tensor_tensor(
                out=by_token[:, v, tokens, :], in0=pairs(u),
                in1=weights.to_broadcast([P, CHUNK, PAIR]), op=ALU.mult,
            )

        def mix_unit(u):
            k, v = divmod(u, UNITS)
            b, c = divmod(k, CHUNKS)
            earlier = slice(PAD - 1 + CHUNK * c, PAD - 1 + CHUNK * (c + 1))
            for e in range(PAIR):
                cb = PAIR * v + e
                nc.vector.scalar_tensor_tensor(
                    out=planes[:, cb, CHUNK * c : CHUNK * (c + 1)], in0=pairs(u)[:, :, e],
                    scalar=keep_share[:, cb : cb + 1],
                    in1=by_channel[:, cb, earlier] if b == 0 or u == SCALAR_UNIT
                    else by_token[:, v, earlier, e],
                    op0=ALU.mult, op1=ALU.add,
                )
            if v == UNITS // 2 - 1 and k > 0:
                regroup_by_gpsimd(c, 0)
            if v == UNITS - 1:
                for g in range(0 if k == 0 else 1, PASSES):
                    regroup_by_vector(c, g)
                for g in range(PASSES):
                    quantise_x(b, c, g)

        def planes_of(c, g):
            return planes[:, PACK * g : PACK * (g + 1), CHUNK * c : CHUNK * (c + 1)]

        def regroup_by_gpsimd(c, g):
            nc.gpsimd.tensor_scalar(
                out=grouped[:, g, CHUNK * c : CHUNK * (c + 1), :],
                in0=planes_of(c, g).rearrange("p j t -> p t j"),
                scalar1=1.0, scalar2=0.0, op0=ALU.mult, op1=ALU.add,
            )

        def regroup_by_vector(c, g):
            nc.vector.tensor_copy(
                out=grouped[:, g, CHUNK * c : CHUNK * (c + 1), :].rearrange(
                    "p (t i) j -> p t j i", i=4
                ),
                in_=planes_of(c, g).rearrange("p j (t i) -> p t j i", i=4),
            )

        def quantise_x(b, c, g):
            if b not in xw_codes:
                xw_codes[b] = codes_pool.tile(
                    [P, PASSES, T], U32, name="xw_codes", tag="xw_codes", align_bytes=64
                )
                xw_scales[b] = codes_pool.tile(
                    [P, PASSES, T], U8, name="xw_scales", tag="xw_scales", align_bytes=64
                )
            tokens = slice(CHUNK * c, CHUNK * (c + 1))
            nc.vector.quantize_mx(
                out=xw_codes[b][:, g, tokens].bitcast(FP8X4),
                scales=xw_scales[b][:, g, tokens],
                in_=grouped[:, g, tokens, :].rearrange("p t j -> p (t j)"),
            )

        mixed = [0]

        def advance():
            u = mixed[0]
            mixed[0] = u + 1
            k, v = divmod(u, UNITS)
            if u > UNITS:
                transpose_unit(u + AHEAD)
            if v == 0 and k + X_BUFS < B * CHUNKS:
                load_x(k + X_BUFS)
            scale_unit(u + 1)
            mix_unit(u)

        h_grouped = {}
        h_codes = {}
        h_scales = {}
        gate = {}

        def hidden(k, i):
            b, c = divmod(k, CHUNKS)
            if i == 0:
                h_grouped[k] = codes_pool.tile(
                    [P, CHUNK, PACK], BF16, name="h_grouped", tag="h_grouped", align_bytes=64
                )
            acc = psum_acc.tile([P, PACK, P], F32, name="h_acc", tag="acc")
            tokens = slice(CHUNK * c + P * i, CHUNK * c + P * (i + 1))
            for m in range(PACK):
                for g in range(PASSES):
                    nc.tensor.matmul_mx(
                        out=acc[:, m, :],
                        lhsT=w1_codes[:, g, P * m : P * (m + 1)].bitcast(FP8X4),
                        lhsT_scale=w1_scales[:, g, P * m : P * (m + 1)],
                        rhs=xw_codes[b][:, g, tokens].bitcast(FP8X4),
                        rhs_scale=xw_scales[b][:, g, tokens],
                        start=(g == 0),
                        stop=(g == PASSES - 1),
                    )
            nc.scalar.activation(
                out=h_grouped[k][:, P * i : P * (i + 1), :],
                in_=acc[:].rearrange("p m t -> p t m"),
                func=ACT.Tanh,
            )

        def quantise_hidden(k):
            h_codes[k] = codes_pool.tile(
                [P, CHUNK], U32, name="h_codes", tag="h_codes", align_bytes=64
            )
            h_scales[k] = codes_pool.tile(
                [P, CHUNK], U8, name="h_scales", tag="h_scales", align_bytes=64
            )
            nc.vector.quantize_mx(
                out=h_codes[k][:].bitcast(FP8X4),
                scales=h_scales[k][:],
                in_=h_grouped[k][:].rearrange("p t j -> p (t j)"),
            )

        def gates(k, cs):
            if cs == 0:
                gate[k] = gate_pool.tile(
                    [P, C_BLOCKS, CHUNK], F32, name="gate", tag="gate", align_bytes=64
                )
            acc = psum_acc.tile([P, CHUNK], F32, name="z_acc", tag="acc")
            nc.tensor.matmul_mx(
                out=acc[:],
                lhsT=w2_codes[:, P * cs : P * (cs + 1)].bitcast(FP8X4),
                lhsT_scale=w2_scales[:, P * cs : P * (cs + 1)],
                rhs=h_codes[k][:].bitcast(FP8X4),
                rhs_scale=h_scales[k][:],
                start=True,
                stop=True,
            )
            nc.scalar.activation(
                out=gate[k][:, cs, :], in_=acc[:], func=ACT.Sigmoid, bias=bias[:, cs : cs + 1],
                scale=1.0,
            )

        results = {}

        def output(k, i, half):
            b, c = divmod(k, CHUNKS)
            if half == 0:
                results[i] = res_pool.tile([P, C], F32, name="result", tag="result")
            acc = psum_acc.tile([P, BANK], F32, name="o_acc", tag="acc")
            for j in range(BANK // P):
                block = gate[k][:, (BANK // P) * half + j, P * i : P * (i + 1)]
                if j == 0:
                    nc.tensor.matmul(
                        out=acc[:, 0:P], lhsT=block, rhs=ident_f32[:], start=True, stop=True
                    )
                else:
                    nc.tensor.transpose(
                        out=acc[:, P * j : P * (j + 1)], in_=block, identity=ident_f32[:]
                    )
            channels = slice(BANK * half, BANK * (half + 1))
            nc.scalar.activation(
                out=results[i][:, channels], in_=acc[:], func=ACT.Ln, scale=math.exp(-0.5)
            )
            rows = slice(CHUNK * c + P * i, CHUNK * c + P * (i + 1))
            if k == B * CHUNKS - 1 and i == TILES - 1:
                nc.sync.dma_start(out=out[b, rows, channels], in_=results[i][:, channels])
            elif half == 1:
                nc.sync.dma_start(out=out[b, rows, :], in_=results[i][:])

        for u in range(UNITS):
            transpose_unit(u)
        for u in range(UNITS):
            scale_unit(u)
        w1_planes = w1_raw.rearrange("p (g j) n -> p g n j", j=PACK)
        nc.gpsimd.tensor_scalar(
            out=w1_grouped[:, 1], in0=w1_planes[:, 1], scalar1=1.0, scalar2=0.0, op0=ALU.mult,
            op1=ALU.add,
        )
        nc.scalar.copy(out=w1_grouped[:, 0], in_=w1_planes[:, 0])
        for u in range(UNITS):
            mix_unit(u)
            transpose_unit(UNITS + u)
        mixed[0] = UNITS
        for g in range(PASSES):
            nc.vector.quantize_mx(
                out=w1_codes[:, g, :].bitcast(FP8X4),
                scales=w1_scales[:, g, :],
                in_=w1_grouped[:, g].rearrange("p n j -> p (n j)"),
            )
        nc.scalar.copy(out=w2_grouped[:, 0 : C // 2], in_=w2_raw[:, 0 : C // 2])
        nc.vector.tensor_copy(
            out=w2_grouped[:, C // 2 : C].rearrange("p (c i) j -> p c j i", i=4),
            in_=w2_raw[:, C // 2 : C].rearrange("p (c i) j -> p c j i", i=4),
        )
        scale_unit(UNITS)

        credit = [0.0]

        def feed(scalar_banks):
            credit[0] += scalar_banks
            while credit[0] >= BANKS_A_UNIT and mixed[0] < last_unit:
                credit[0] -= BANKS_A_UNIT
                advance()

        def steps(chunks):
            tanh = [[("h", k, i) for i in range(TILES)] + [("q", k, 0)] for k in chunks]
            sigmoid = [[("z", k, cs) for cs in range(C_BLOCKS)] for k in chunks]
            if len(chunks) == 2:
                return tanh[0] + sigmoid[0] + tanh[1] + sigmoid[1]
            free = C_BLOCKS - HELD
            return (
                tanh[0] + tanh[1] + sigmoid[0]
                + sigmoid[1][:free] + tanh[2] + sigmoid[1][free:] + sigmoid[2]
            )

        for r, chunks in enumerate(ROUNDS):
            if r > 0:
                feed(TABLE_BANKS)
                nc.scalar.activation(out=table_warm[:], in_=columns[:, 0:1], func=ACT.Sigmoid)
            for n, (kind, k, i) in enumerate(steps(chunks)):
                if r == 0:
                    chunk, position = divmod(n, TILES + 1 + C_BLOCKS)
                    if position in FIRST_ROUND[chunk]:
                        advance()
                elif kind != "q":
                    feed(1)
                if kind == "h":
                    while mixed[0] < UNITS * (k + 1):
                        advance()
                    hidden(k, i)
                elif kind == "q":
                    if k == 0:
                        nc.vector.quantize_mx(
                            out=w2_codes[:].bitcast(FP8X4),
                            scales=w2_scales[:],
                            in_=w2_grouped.rearrange("p c j -> p (c j)"),
                        )
                    quantise_hidden(k)
                else:
                    gates(k, i)
            feed(TABLE_BANKS)
            for k in chunks:
                for i in range(TILES):
                    for half in range(C // BANK):
                        feed(1)
                        output(k, i, half)
